import numpy as np
import ml_dtypes


def mxq(x, axis, fmt="e4m3"):
    dtype, down = {"e4m3": (ml_dtypes.float8_e4m3fn, 7), "e5m2": (ml_dtypes.float8_e5m2, 14)}[fmt]
    v = np.moveaxis(np.asarray(x, np.float32).astype(ml_dtypes.bfloat16).astype(np.float64), axis, -1)
    blocks = v.reshape(v.shape[:-1] + (-1, 32))
    amax = np.abs(blocks).max(-1, keepdims=True)
    byte = np.maximum(np.where(amax > 0, np.frexp(amax)[1] - 1 + 127, 0) - down, 1)
    scale = np.exp2(byte - 127.0)
    codes = (blocks / scale).astype(np.float32).astype(dtype).astype(np.float64)
    return np.moveaxis((codes * scale).reshape(v.shape), -1, axis)


WIDE = False


def mx_kscale(k):
    if not WIDE:
        return np.ones(k)
    levels = np.array([20, -20, 10, -10, 0])
    a = np.random.permutation(np.resize(levels, k // 512 * 4)).reshape(k // 512, 4)
    idx = np.arange(k)
    return np.exp2(a[idx // 512, idx % 128 // 32])


BF16 = ml_dtypes.bfloat16


def bf(x):
    return np.asarray(x, np.float32).astype(BF16)


def f64(x):
    return np.asarray(x).astype(np.float64)


B, C, H, W, M, O = 16, 512, 16, 16, 512, 512
N = B * H * W
L2_EPS = 1e-12
BN_EPS = 1e-5


def l2_normalize(x, axis):
    n = np.sqrt(np.sum(x * x, axis=axis, keepdims=True))
    return x / np.maximum(n, L2_EPS)


def conv_stats(query, concat_memory, conv_w):
    q_flat = l2_normalize(f64(query), 1).transpose(0, 2, 3, 1).reshape(N, C)
    y = np.concatenate([q_flat, f64(concat_memory)], axis=1) @ f64(conv_w).T
    mean = np.mean(y, axis=0)
    var = np.mean((y - mean) ** 2, axis=0)
    return y, mean, var


def setup_inputs():
    u = mx_kscale(O)
    cm = bf((np.random.standard_normal((N, C)) * 5.0 + np.random.standard_normal((1, C)) * 1.5) / np.sqrt(C))
    w0 = bf(np.random.standard_normal((O, 2 * C)) * 0.1 / np.sqrt(2 * C))
    query = bf(np.random.standard_normal((B, C, H, W)))
    gamma = bf(1.0 + 0.1 * np.random.standard_normal(O))
    beta = bf(0.2 * np.random.standard_normal(O))
    g = np.random.standard_normal((B, O, H, W)) * np.exp2(np.random.randint(-12, 1, (B, 1, H, W))) * 64.0
    g = bf(g * u[None, :, None, None])
    y, mean, var = conv_stats(query, cm, w0)
    return {"query": query, "concat_memory": cm, "conv_w": bf(f64(w0) / u[:, None]),
            "bn_gamma": gamma, "bn_beta": beta,
            "y_conv": np.asarray(y, np.float32), "bn_mean": np.asarray(mean, np.float32),
            "bn_var": np.asarray(var, np.float32), "grad_out": g}


def reference(query, concat_memory, conv_w, bn_gamma, bn_beta, y_conv, bn_mean, bn_var, grad_out):
    g = f64(grad_out).transpose(0, 2, 3, 1).reshape(N, O)
    gam = f64(bn_gamma)
    rstd = 1.0 / np.sqrt(f64(bn_var) + BN_EPS)
    xhat = (f64(y_conv) - f64(bn_mean)) * rstd
    dxh = np.where(xhat * gam + f64(bn_beta) > 0.0, g, 0.0) * gam
    m1 = np.mean(dxh, axis=0)
    m2 = np.mean(dxh * xhat, axis=0)
    dy = (dxh - m1 - xhat * m2) * rstd
    dqf = mxq(dy, 1, "e5m2") @ mxq(f64(conv_w)[:, :C], 0, "e4m3")
    dq = dqf.reshape(B, H, W, C).transpose(0, 3, 1, 2)
    qr = f64(query)
    nrm = np.maximum(np.sqrt(np.sum(qr * qr, axis=1, keepdims=True)), L2_EPS)
    q = qr / nrm
    return (dq - q * np.sum(q * dq, axis=1, keepdims=True)) / nrm

@@ -1,0 +1,279 @@
+import concourse.mybir as mybir
+from concourse.masks import make_identity
+
+F32 = mybir.dt.float32
+BF16 = mybir.dt.bfloat16
+U32 = mybir.dt.uint32
+U8 = mybir.dt.uint8
+E4M3_X4 = mybir.dt.float8_e4m3fn_x4
+E5M2_X4 = mybir.dt.float8_e5m2_x4
+ALU = mybir.AluOpType
+ACT = mybir.ActivationFunctionType
+AXIS = mybir.AxisListType
+
+P = 128
+PACK = 4
+IMAGES = 16
+CHANNELS = P * PACK
+IMAGE_PIXELS = 256
+PIXELS = IMAGES * IMAGE_PIXELS
+GROUP_IMAGES = 2
+GROUP_PIXELS = GROUP_IMAGES * IMAGE_PIXELS
+GROUPS = IMAGES // GROUP_IMAGES
+HALVES = IMAGE_PIXELS // P
+BLOCKS = GROUP_PIXELS // P
+BN_EPS = 1e-5
+L2_EPS = 1e-12
+TINY = 1e-30
+
+FLOPS = 2 * PIXELS * CHANNELS * CHANNELS
+BYTES = (
+    2 * PIXELS * CHANNELS
+    + 2 * CHANNELS * CHANNELS
+    + 4 * PIXELS * CHANNELS
+    + 2 * PIXELS * CHANNELS
+    + 4 * PIXELS * CHANNELS
+)
+
+
+def tile_memory_sup_pb_v_kernel(
+    tc, query, concat_memory, conv_w, bn_gamma, bn_beta, y_conv, bn_mean, bn_var, grad_out, out
+):
+    nc = tc.nc
+
+    y_groups = y_conv.rearrange("(g k p) o -> g p k o", k=BLOCKS, p=P)
+    grad_groups = grad_out.rearrange("(g b) (p t) h w -> g p b (t h w)", b=GROUP_IMAGES, t=PACK)
+    query_groups = query.rearrange("(g b) (p t) h w -> g p b (t h w)", b=GROUP_IMAGES, t=PACK)
+    out_groups = out.rearrange("(g b) (p t) h w -> g p b (t h w)", b=GROUP_IMAGES, t=PACK)
+
+    with tc.tile_pool(name="const", bufs=1) as const, tc.tile_pool(name="resident", bufs=1) as resident:
+        var = const.tile([P, PACK], F32)
+        mean = const.tile([P, PACK], F32)
+        gamma_bf = const.tile([P, PACK], BF16)
+        beta_bf = const.tile([P, PACK], BF16)
+        nc.scalar.dma_start(out=var[:], in_=bn_var.rearrange("(p t) -> p t", t=PACK))
+        nc.scalar.dma_start(out=gamma_bf[:], in_=bn_gamma.rearrange("(p t) -> p t", t=PACK))
+        nc.scalar.dma_start(out=mean[:], in_=bn_mean.rearrange("(p t) -> p t", t=PACK))
+        nc.scalar.dma_start(out=beta_bf[:], in_=bn_beta.rearrange("(p t) -> p t", t=PACK))
+        w_rows = const.tile([P, PACK, CHANNELS], BF16)
+        nc.scalar.dma_start(out=w_rows[:], in_=conv_w[:, 0:CHANNELS].rearrange("(p j) c -> p j c", j=PACK))
+
+        ident_f32 = const.tile([P, P], F32)
+        make_identity(nc, ident_f32[:])
+        ident_bf16 = const.tile([P, P], BF16)
+        make_identity(nc, ident_bf16[:])
+
+        var_eps = const.tile([P, PACK], F32)
+        nc.vector.tensor_scalar_add(out=var_eps[:], in0=var[:], scalar1=BN_EPS)
+        sd_rough = const.tile([P, PACK], F32)
+        nc.scalar.sqrt(out=sd_rough[:], in_=var_eps[:])
+        sd = const.tile([P, PACK], F32)
+        nc.vector.reciprocal(out=sd[:], in_=sd_rough[:])
+        nc.vector.tensor_mul(out=sd[:], in0=sd[:], in1=var_eps[:])
+        nc.vector.tensor_add(out=sd[:], in0=sd[:], in1=sd_rough[:])
+        nc.vector.tensor_scalar_mul(out=sd[:], in0=sd[:], scalar1=0.5)
+        rstd = const.tile([P, PACK], F32)
+        nc.vector.reciprocal(out=rstd[:], in_=sd[:])
+
+        gamma = const.tile([P, PACK], F32)
+        nc.vector.tensor_copy(out=gamma[:], in_=gamma_bf[:])
+        sign = const.tile([P, PACK], F32)
+        nc.vector.tensor_single_scalar(out=sign[:], in_=gamma[:], scalar=0.0, op=ALU.is_lt)
+        nc.vector.scalar_tensor_tensor(
+            out=sign[:], in0=gamma[:], scalar=0.0, in1=sign[:], op0=ALU.is_gt, op1=ALU.subtract
+        )
+        shift = const.tile([P, PACK], F32)
+        nc.vector.scalar_tensor_tensor(
+            out=shift[:], in0=mean[:], scalar=-1.0, in1=sign[:], op0=ALU.mult, op1=ALU.mult
+        )
+        threshold = const.tile([P, PACK], F32)
+        nc.vector.scalar_tensor_tensor(
+            out=threshold[:], in0=gamma[:], scalar=-1.0, in1=gamma[:], op0=ALU.mult, op1=ALU.max
+        )
+        nc.vector.tensor_scalar_max(out=threshold[:], in0=threshold[:], scalar1=TINY)
+        nc.vector.reciprocal(out=threshold[:], in_=threshold[:])
+        nc.vector.tensor_mul(out=threshold[:], in0=threshold[:], in1=sd[:])
+        nc.vector.scalar_tensor_tensor(
+            out=threshold[:], in0=beta_bf[:], scalar=-1.0, in1=threshold[:], op0=ALU.mult, op1=ALU.mult
+        )
+        gain = const.tile([P, PACK], F32)
+        nc.vector.tensor_mul(out=gain[:], in0=gamma[:], in1=rstd[:])
+        sum1_to_offset = const.tile([P, PACK], F32)
+        nc.vector.tensor_scalar_mul(out=sum1_to_offset[:], in0=gain[:], scalar1=-1.0 / PIXELS)
+        sum2_to_slope = const.tile([P, PACK], F32)
+        nc.vector.tensor_mul(out=sum2_to_slope[:], in0=sum1_to_offset[:], in1=rstd[:])
+        nc.vector.tensor_mul(out=sum2_to_slope[:], in0=sum2_to_slope[:], in1=rstd[:])
+
+        sum1_parts = const.tile([P, PACK, GROUPS], F32)
+        sum2_parts = const.tile([P, PACK, GROUPS], F32)
+        norm2 = const.tile([P, GROUPS * BLOCKS], F32)
+
+        ds = []
+        masked = []
+        query_sb = []
+
+        with tc.tile_pool(name="stage1", bufs=3) as stage1, tc.psum_pool(name="psum1", bufs=4) as psum1:
+            for g in range(GROUPS):
+                y_sb = stage1.tile([P, BLOCKS, CHANNELS], F32)
+                nc.sync.dma_start(out=y_sb[:], in_=y_groups[g])
+                masked_g = resident.tile([P, GROUP_IMAGES, PACK, IMAGE_PIXELS], BF16, name="masked%d" % g)
+                nc.sync.dma_start(out=masked_g[:].rearrange("p b t n -> p b (t n)"), in_=grad_groups[g])
+                query_g = resident.tile([P, GROUP_IMAGES, PACK, IMAGE_PIXELS], BF16, name="query%d" % g)
+                nc.sync.dma_start(out=query_g[:].rearrange("p b t n -> p b (t n)"), in_=query_groups[g])
+                ds_g = resident.tile([P, PACK, GROUP_PIXELS], F32, name="ds%d" % g)
+                ds.append(ds_g)
+                masked.append(masked_g)
+                query_sb.append(query_g)
+
+                y_by_slot = y_sb[:].rearrange("p k (c t) -> p k t c", t=PACK)
+                for t in range(PACK):
+                    y_t = psum1.tile([P, GROUP_PIXELS], F32, tag="y_t")
+                    for k in range(BLOCKS):
+                        nc.tensor.transpose(y_t[:, k * P : (k + 1) * P], y_by_slot[:, k, t, :], ident_f32[:])
+                    nc.scalar.activation(
+                        out=ds_g[:, t, :], in_=y_t[:], func=ACT.Identity,
+                        bias=shift[:, t : t + 1], scale=sign[:, t : t + 1],
+                    )
+                for t in range(PACK):
+                    nc.vector.scalar_tensor_tensor(
+                        out=masked_g[:, :, t, :],
+                        in0=ds_g[:, t, :].rearrange("p (b n) -> p b n", b=GROUP_IMAGES),
+                        scalar=threshold[:, t : t + 1],
+                        in1=masked_g[:, :, t, :],
+                        op0=ALU.is_gt, op1=ALU.mult,
+                        accum_out=sum1_parts[:, t, g : g + 1],
+                    )
+                for t in range(PACK):
+                    product = stage1.tile([P, GROUP_IMAGES, IMAGE_PIXELS], BF16, tag="product", bufs=4)
+                    nc.vector.scalar_tensor_tensor(
+                        out=product[:],
+                        in0=ds_g[:, t, :].rearrange("p (b n) -> p b n", b=GROUP_IMAGES),
+                        scalar=1.0,
+                        in1=masked_g[:, :, t, :],
+                        op0=ALU.mult, op1=ALU.mult,
+                        accum_out=sum2_parts[:, t, g : g + 1],
+                    )
+
+                for b in range(GROUP_IMAGES):
+                    query_t = psum1.tile([P, HALVES, CHANNELS], BF16, tag="query_t")
+                    for h in range(HALVES):
+                        for t in range(PACK):
+                            nc.tensor.transpose(
+                                query_t[:, h, t * P : (t + 1) * P],
+                                query_g[:, b, t, h * P : (h + 1) * P],
+                                ident_bf16[:],
+                            )
+                    for h in range(HALVES):
+                        block = (g * GROUP_IMAGES + b) * HALVES + h
+                        square = stage1.tile([P, CHANNELS], BF16, tag="square", bufs=4)
+                        nc.scalar.activation(
+                            out=square[:], in_=query_t[:, h, :], func=ACT.Square,
+                            accum_out=norm2[:, block : block + 1],
+                        )
+
+        sum1 = const.tile([P, PACK], F32)
+        nc.vector.tensor_reduce(out=sum1[:], in_=sum1_parts[:], axis=AXIS.X, op=ALU.add)
+        sum2 = const.tile([P, PACK], F32)
+        nc.vector.tensor_reduce(out=sum2[:], in_=sum2_parts[:], axis=AXIS.X, op=ALU.add)
+        offset = const.tile([P, PACK], F32)
+        nc.vector.tensor_mul(out=offset[:], in0=sum1[:], in1=sum1_to_offset[:])
+        slope = const.tile([P, PACK], F32)
+        nc.vector.tensor_mul(out=slope[:], in0=sum2[:], in1=sum2_to_slope[:])
+
+        inv_norm = const.tile([P, GROUPS * BLOCKS], F32)
+        nc.scalar.sqrt(out=inv_norm[:], in_=norm2[:])
+        nc.vector.tensor_scalar_max(out=inv_norm[:], in0=inv_norm[:], scalar1=L2_EPS)
+        nc.vector.reciprocal(out=inv_norm[:], in_=inv_norm[:])
+        neg_inv_norm2 = const.tile([P, GROUPS * BLOCKS], F32)
+        nc.vector.scalar_tensor_tensor(
+            out=neg_inv_norm2[:], in0=inv_norm[:], scalar=-1.0, in1=inv_norm[:], op0=ALU.mult, op1=ALU.mult
+        )
+
+        w_words_bf = const.tile([P, CHANNELS, PACK], BF16, align_bytes=64)
+        nc.vector.tensor_copy(
+            out=w_words_bf[:].rearrange("p (t c) j -> p t c j", t=PACK),
+            in_=w_rows[:].rearrange("p j (c t) -> p t c j", t=PACK),
+        )
+        w_codes = const.tile([P, CHANNELS], U32, align_bytes=64)
+        w_scales = const.tile([P, CHANNELS], U8, align_bytes=64)
+        nc.vector.quantize_mx(
+            out=w_codes[:].bitcast(E4M3_X4), scales=w_scales[:], in_=w_words_bf[:].rearrange("p c j -> p (c j)")
+        )
+
+        with tc.tile_pool(name="stage2", bufs=2) as stage2, tc.psum_pool(name="psum2", bufs=2) as psum2:
+            for g in range(GROUPS):
+                for t in range(PACK):
+                    nc.scalar.activation(
+                        out=ds[g][:, t, :], in_=ds[g][:, t, :], func=ACT.Identity,
+                        bias=offset[:, t : t + 1], scale=slope[:, t : t + 1],
+                    )
+                dy_rows = stage2.tile([P, PACK, GROUP_PIXELS], BF16)
+                for t in range(PACK):
+                    nc.vector.scalar_tensor_tensor(
+                        out=dy_rows[:, t, :].rearrange("p (b n) -> p b n", b=GROUP_IMAGES),
+                        in0=masked[g][:, :, t, :],
+                        scalar=gain[:, t : t + 1],
+                        in1=ds[g][:, t, :].rearrange("p (b n) -> p b n", b=GROUP_IMAGES),
+                        op0=ALU.mult, op1=ALU.add,
+                    )
+                dy_words_bf = stage2.tile([P, GROUP_PIXELS, PACK], BF16, align_bytes=64)
+                nc.vector.tensor_copy(
+                    out=dy_words_bf[:].rearrange("p (c i) t -> p c t i", i=4),
+                    in_=dy_rows[:].rearrange("p t (c i) -> p c t i", i=4),
+                )
+                dy_codes = stage2.tile([P, GROUP_PIXELS], U32, align_bytes=64)
+                dy_scales = stage2.tile([P, GROUP_PIXELS], U8, align_bytes=64)
+                nc.vector.quantize_mx(
+                    out=dy_codes[:].bitcast(E5M2_X4), scales=dy_scales[:],
+                    in_=dy_words_bf[:].rearrange("p n t -> p (n t)"),
+                )
+
+                query_t = []
+                for b in range(GROUP_IMAGES):
+                    query_t_b = psum2.tile([P, HALVES, CHANNELS], BF16, tag="query_t", bufs=3)
+                    for h in range(HALVES):
+                        for t in range(PACK):
+                            nc.tensor.transpose(
+                                query_t_b[:, h, t * P : (t + 1) * P],
+                                query_sb[g][:, b, t, h * P : (h + 1) * P],
+                                ident_bf16[:],
+                            )
+                    query_t.append(query_t_b)
+
+                dot = stage2.tile([P, BLOCKS], F32)
+                scaled = []
+                for k in range(BLOCKS):
+                    block = g * BLOCKS + k
+                    dq = psum2.tile([P, CHANNELS], F32, tag="dq", bufs=2)
+                    nc.tensor.matmul_mx(
+                        out=dq[:],
+                        lhsT=dy_codes[:, k * P : (k + 1) * P].bitcast(E5M2_X4),
+                        lhsT_scale=dy_scales[:, k * P : (k + 1) * P],
+                        rhs=w_codes[:].bitcast(E4M3_X4),
+                        rhs_scale=w_scales[:],
+                        start=True, stop=True,
+                    )
+                    scaled_k = stage2.tile([P, CHANNELS], F32, tag="scaled", bufs=2 * BLOCKS)
+                    nc.scalar.activation(
+                        out=scaled_k[:], in_=dq[:], func=ACT.Copy, scale=inv_norm[:, block : block + 1]
+                    )
+                    scaled.append(scaled_k)
+                    product = stage2.tile([P, CHANNELS], BF16, tag="product", bufs=4)
+                    nc.vector.scalar_tensor_tensor(
+                        out=product[:], in0=scaled_k[:], scalar=1.0, in1=query_t[k // HALVES][:, k % HALVES, :],
+                        op0=ALU.mult, op1=ALU.mult, accum_out=dot[:, k : k + 1],
+                    )
+                weight = stage2.tile([P, BLOCKS], F32)
+                nc.vector.tensor_mul(out=weight[:], in0=dot[:], in1=neg_inv_norm2[:, g * BLOCKS : (g + 1) * BLOCKS])
+                out_sb = stage2.tile([P, GROUP_IMAGES, PACK, IMAGE_PIXELS], F32)
+                for k in range(BLOCKS):
+                    nc.vector.scalar_tensor_tensor(
+                        out=scaled[k][:], in0=query_t[k // HALVES][:, k % HALVES, :], scalar=weight[:, k : k + 1],
+                        in1=scaled[k][:], op0=ALU.mult, op1=ALU.add,
+                    )
+                    out_t = psum2.tile([P, PACK, P], F32, tag="out_t", bufs=3)
+                    for t in range(PACK):
+                        nc.tensor.transpose(out_t[:, t, :], scaled[k][:, t * P : (t + 1) * P], ident_f32[:])
+                    first = (k % HALVES) * P
+                    nc.scalar.copy(out=out_sb[:, k // HALVES, :, first : first + P], in_=out_t[:])
+                nc.sync.dma_start(out=out_groups[g], in_=out_sb[:].rearrange("p b t n -> p b (t n)"))

@@ -20,6 +20,7 @@ PIXELS = IMAGES * IMAGE_PIXELS
 GROUP_IMAGES = 2
 GROUP_PIXELS = GROUP_IMAGES * IMAGE_PIXELS
 GROUPS = IMAGES // GROUP_IMAGES
+PAIR = 2
 HALVES = IMAGE_PIXELS // P
 BLOCKS = GROUP_PIXELS // P
 BN_EPS = 1e-5
@@ -116,13 +117,19 @@ def tile_memory_sup_pb_v_kernel(
             for g in range(GROUPS):
                 y_sb = stage1.tile([P, BLOCKS, CHANNELS], F32)
                 nc.sync.dma_start(out=y_sb[:], in_=y_groups[g])
-                masked_g = resident.tile([P, GROUP_IMAGES, PACK, IMAGE_PIXELS], BF16, name="masked%d" % g)
-                nc.sync.dma_start(out=masked_g[:].rearrange("p b t n -> p b (t n)"), in_=grad_groups[g])
+                member = g % PAIR
+                if member == 0:
+                    masked_pair = resident.tile(
+                        [P, PAIR * GROUP_IMAGES, PACK, IMAGE_PIXELS], BF16, name="masked%d" % (g // PAIR)
+                    )
+                    ds_pair = resident.tile([P, PACK, PAIR * GROUP_PIXELS], F32, name="ds%d" % (g // PAIR))
+                    masked.append(masked_pair)
+                    ds.append(ds_pair)
+                masked_g = masked_pair[:, member * GROUP_IMAGES : (member + 1) * GROUP_IMAGES, :, :]
+                ds_g = ds_pair[:, :, member * GROUP_PIXELS : (member + 1) * GROUP_PIXELS]
+                nc.sync.dma_start(out=masked_g.rearrange("p b t n -> p b (t n)"), in_=grad_groups[g])
                 query_g = resident.tile([P, GROUP_IMAGES, PACK, IMAGE_PIXELS], BF16, name="query%d" % g)
                 nc.sync.dma_start(out=query_g[:].rearrange("p b t n -> p b (t n)"), in_=query_groups[g])
-                ds_g = resident.tile([P, PACK, GROUP_PIXELS], F32, name="ds%d" % g)
-                ds.append(ds_g)
-                masked.append(masked_g)
                 query_sb.append(query_g)
 
                 y_by_slot = y_sb[:].rearrange("p k (c t) -> p k t c", t=PACK)
@@ -201,79 +208,81 @@ def tile_memory_sup_pb_v_kernel(
         )
 
         with tc.tile_pool(name="stage2", bufs=2) as stage2, tc.psum_pool(name="psum2", bufs=2) as psum2:
-            for g in range(GROUPS):
+            for pair in range(GROUPS // PAIR):
+                members = [pair * PAIR + i for i in range(PAIR)]
                 for t in range(PACK):
                     nc.scalar.activation(
-                        out=ds[g][:, t, :], in_=ds[g][:, t, :], func=ACT.Identity,
+                        out=ds[pair][:, t, :], in_=ds[pair][:, t, :], func=ACT.Identity,
                         bias=offset[:, t : t + 1], scale=slope[:, t : t + 1],
                     )
-                dy_rows = stage2.tile([P, PACK, GROUP_PIXELS], BF16)
+                dy_rows = stage2.tile([P, PACK, PAIR * GROUP_PIXELS], BF16)
                 for t in range(PACK):
                     nc.vector.scalar_tensor_tensor(
-                        out=dy_rows[:, t, :].rearrange("p (b n) -> p b n", b=GROUP_IMAGES),
-                        in0=masked[g][:, :, t, :],
+                        out=dy_rows[:, t, :].rearrange("p (b n) -> p b n", n=IMAGE_PIXELS),
+                        in0=masked[pair][:, :, t, :],
                         scalar=gain[:, t : t + 1],
-                        in1=ds[g][:, t, :].rearrange("p (b n) -> p b n", b=GROUP_IMAGES),
+                        in1=ds[pair][:, t, :].rearrange("p (b n) -> p b n", n=IMAGE_PIXELS),
                         op0=ALU.mult, op1=ALU.add,
                     )
-                dy_words_bf = stage2.tile([P, GROUP_PIXELS, PACK], BF16, align_bytes=64)
+                dy_words_bf = stage2.tile([P, PAIR * GROUP_PIXELS, PACK], BF16, align_bytes=64)
                 nc.vector.tensor_copy(
                     out=dy_words_bf[:].rearrange("p (c i) t -> p c t i", i=4),
                     in_=dy_rows[:].rearrange("p t (c i) -> p c t i", i=4),
                 )
-                dy_codes = stage2.tile([P, GROUP_PIXELS], U32, align_bytes=64)
-                dy_scales = stage2.tile([P, GROUP_PIXELS], U8, align_bytes=64)
+                dy_codes = stage2.tile([P, PAIR * GROUP_PIXELS], U32, align_bytes=64)
+                dy_scales = stage2.tile([P, PAIR * GROUP_PIXELS], U8, align_bytes=64)
                 nc.vector.quantize_mx(
                     out=dy_codes[:].bitcast(E5M2_X4), scales=dy_scales[:],
                     in_=dy_words_bf[:].rearrange("p n t -> p (n t)"),
                 )
 
-                query_t = []
-                for b in range(GROUP_IMAGES):
-                    query_t_b = psum2.tile([P, HALVES, CHANNELS], BF16, tag="query_t", bufs=3)
-                    for h in range(HALVES):
-                        for t in range(PACK):
-                            nc.tensor.transpose(
-                                query_t_b[:, h, t * P : (t + 1) * P],
-                                query_sb[g][:, b, t, h * P : (h + 1) * P],
-                                ident_bf16[:],
-                            )
-                    query_t.append(query_t_b)
+                for i, g in enumerate(members):
+                    query_t = []
+                    for b in range(GROUP_IMAGES):
+                        query_t_b = psum2.tile([P, HALVES, CHANNELS], BF16, tag="query_t", bufs=3)
+                        for h in range(HALVES):
+                            for t in range(PACK):
+                                nc.tensor.transpose(
+                                    query_t_b[:, h, t * P : (t + 1) * P],
+                                    query_sb[g][:, b, t, h * P : (h + 1) * P],
+                                    ident_bf16[:],
+                                )
+                        query_t.append(query_t_b)
 
-                dot = stage2.tile([P, BLOCKS], F32)
-                scaled = []
-                for k in range(BLOCKS):
-                    block = g * BLOCKS + k
-                    dq = psum2.tile([P, CHANNELS], F32, tag="dq", bufs=2)
-                    nc.tensor.matmul_mx(
-                        out=dq[:],
-                        lhsT=dy_codes[:, k * P : (k + 1) * P].bitcast(E5M2_X4),
-                        lhsT_scale=dy_scales[:, k * P : (k + 1) * P],
-                        rhs=w_codes[:].bitcast(E4M3_X4),
-                        rhs_scale=w_scales[:],
-                        start=True, stop=True,
-                    )
-                    scaled_k = stage2.tile([P, CHANNELS], F32, tag="scaled", bufs=2 * BLOCKS)
-                    nc.scalar.activation(
-                        out=scaled_k[:], in_=dq[:], func=ACT.Copy, scale=inv_norm[:, block : block + 1]
-                    )
-                    scaled.append(scaled_k)
-                    product = stage2.tile([P, CHANNELS], BF16, tag="product", bufs=4)
-                    nc.vector.scalar_tensor_tensor(
-                        out=product[:], in0=scaled_k[:], scalar=1.0, in1=query_t[k // HALVES][:, k % HALVES, :],
-                        op0=ALU.mult, op1=ALU.mult, accum_out=dot[:, k : k + 1],
-                    )
-                weight = stage2.tile([P, BLOCKS], F32)
-                nc.vector.tensor_mul(out=weight[:], in0=dot[:], in1=neg_inv_norm2[:, g * BLOCKS : (g + 1) * BLOCKS])
-                out_sb = stage2.tile([P, GROUP_IMAGES, PACK, IMAGE_PIXELS], F32)
-                for k in range(BLOCKS):
-                    nc.vector.scalar_tensor_tensor(
-                        out=scaled[k][:], in0=query_t[k // HALVES][:, k % HALVES, :], scalar=weight[:, k : k + 1],
-                        in1=scaled[k][:], op0=ALU.mult, op1=ALU.add,
-                    )
-                    out_t = psum2.tile([P, PACK, P], F32, tag="out_t", bufs=3)
-                    for t in range(PACK):
-                        nc.tensor.transpose(out_t[:, t, :], scaled[k][:, t * P : (t + 1) * P], ident_f32[:])
-                    first = (k % HALVES) * P
-                    nc.scalar.copy(out=out_sb[:, k // HALVES, :, first : first + P], in_=out_t[:])
-                nc.sync.dma_start(out=out_groups[g], in_=out_sb[:].rearrange("p b t n -> p b (t n)"))
+                    weight = stage2.tile([P, BLOCKS], F32)
+                    scaled = []
+                    for k in range(BLOCKS):
+                        block = g * BLOCKS + k
+                        first_column = (i * BLOCKS + k) * P
+                        dq = psum2.tile([P, CHANNELS], F32, tag="dq", bufs=2)
+                        nc.tensor.matmul_mx(
+                            out=dq[:],
+                            lhsT=dy_codes[:, first_column : first_column + P].bitcast(E5M2_X4),
+                            lhsT_scale=dy_scales[:, first_column : first_column + P],
+                            rhs=w_codes[:].bitcast(E4M3_X4),
+                            rhs_scale=w_scales[:],
+                            start=True, stop=True,
+                        )
+                        scaled_k = stage2.tile([P, CHANNELS], F32, tag="scaled", bufs=2 * BLOCKS)
+                        nc.scalar.activation(
+                            out=scaled_k[:], in_=dq[:], func=ACT.Copy, scale=inv_norm[:, block : block + 1]
+                        )
+                        scaled.append(scaled_k)
+                        product = stage2.tile([P, CHANNELS], BF16, tag="product", bufs=4)
+                        nc.vector.scalar_tensor_tensor(
+                            out=product[:], in0=scaled_k[:], scalar=neg_inv_norm2[:, block : block + 1],
+                            in1=query_t[k // HALVES][:, k % HALVES, :],
+                            op0=ALU.mult, op1=ALU.mult, accum_out=weight[:, k : k + 1],
+                        )
+                    out_sb = stage2.tile([P, GROUP_IMAGES, PACK, IMAGE_PIXELS], F32)
+                    for k in range(BLOCKS):
+                        nc.vector.scalar_tensor_tensor(
+                            out=scaled[k][:], in0=query_t[k // HALVES][:, k % HALVES, :], scalar=weight[:, k : k + 1],
+                            in1=scaled[k][:], op0=ALU.mult, op1=ALU.add,
+                        )
+                        out_t = psum2.tile([P, PACK, P], F32, tag="out_t", bufs=3)
+                        for t in range(PACK):
+                            nc.tensor.transpose(out_t[:, t, :], scaled[k][:, t * P : (t + 1) * P], ident_f32[:])
+                        first = (k % HALVES) * P
+                        nc.scalar.copy(out=out_sb[:, k // HALVES, :, first : first + P], in_=out_t[:])
+                    nc.sync.dma_start(out=out_groups[g], in_=out_sb[:].rearrange("p b t n -> p b (t n)"))

@@ -21,6 +21,8 @@ GROUP_IMAGES = 2
 GROUP_PIXELS = GROUP_IMAGES * IMAGE_PIXELS
 GROUPS = IMAGES // GROUP_IMAGES
 PAIR = 2
+W_LOAD_AFTER_GROUP = 2
+VECTOR_SHARE = 640
 HALVES = IMAGE_PIXELS // P
 BLOCKS = GROUP_PIXELS // P
 BN_EPS = 1e-5
@@ -45,7 +47,7 @@ def tile_memory_sup_pb_v_kernel(
     y_groups = y_conv.rearrange("(g k p) o -> g p k o", k=BLOCKS, p=P)
     grad_groups = grad_out.rearrange("(g b) (p t) h w -> g p b (t h w)", b=GROUP_IMAGES, t=PACK)
     query_groups = query.rearrange("(g b) (p t) h w -> g p b (t h w)", b=GROUP_IMAGES, t=PACK)
-    out_groups = out.rearrange("(g b) (p t) h w -> g p b (t h w)", b=GROUP_IMAGES, t=PACK)
+    out_images = out.rearrange("b (p t) h w -> b p (t h w)", t=PACK)
 
     with tc.tile_pool(name="const", bufs=1) as const, tc.tile_pool(name="resident", bufs=1) as resident:
         var = const.tile([P, PACK], F32)
@@ -57,7 +59,6 @@ def tile_memory_sup_pb_v_kernel(
         nc.scalar.dma_start(out=mean[:], in_=bn_mean.rearrange("(p t) -> p t", t=PACK))
         nc.scalar.dma_start(out=beta_bf[:], in_=bn_beta.rearrange("(p t) -> p t", t=PACK))
         w_rows = const.tile([P, PACK, CHANNELS], BF16)
-        nc.scalar.dma_start(out=w_rows[:], in_=conv_w[:, 0:CHANNELS].rearrange("(p j) c -> p j c", j=PACK))
 
         ident_f32 = const.tile([P, P], F32)
         make_identity(nc, ident_f32[:])
@@ -131,6 +132,10 @@ def tile_memory_sup_pb_v_kernel(
                 query_g = resident.tile([P, GROUP_IMAGES, PACK, IMAGE_PIXELS], BF16, name="query%d" % g)
                 nc.sync.dma_start(out=query_g[:].rearrange("p b t n -> p b (t n)"), in_=query_groups[g])
                 query_sb.append(query_g)
+                if g == W_LOAD_AFTER_GROUP:
+                    nc.sync.dma_start(
+                        out=w_rows[:], in_=conv_w[:, 0:CHANNELS].rearrange("(p j) c -> p j c", j=PACK)
+                    )
 
                 y_by_slot = y_sb[:].rearrange("p k (c t) -> p k t c", t=PACK)
                 for t in range(PACK):
@@ -226,8 +231,12 @@ def tile_memory_sup_pb_v_kernel(
                     )
                 dy_words_bf = stage2.tile([P, PAIR * GROUP_PIXELS, PACK], BF16, align_bytes=64)
                 nc.vector.tensor_copy(
-                    out=dy_words_bf[:].rearrange("p (c i) t -> p c t i", i=4),
-                    in_=dy_rows[:].rearrange("p t (c i) -> p c t i", i=4),
+                    out=dy_words_bf[:, 0:VECTOR_SHARE, :].rearrange("p (c i) t -> p c t i", i=4),
+                    in_=dy_rows[:, :, 0:VECTOR_SHARE].rearrange("p t (c i) -> p c t i", i=4),
+                )
+                nc.scalar.copy(
+                    out=dy_words_bf[:, VECTOR_SHARE:, :],
+                    in_=dy_rows[:, :, VECTOR_SHARE:].rearrange("p t n -> p n t"),
                 )
                 dy_codes = stage2.tile([P, PAIR * GROUP_PIXELS], U32, align_bytes=64)
                 dy_scales = stage2.tile([P, PAIR * GROUP_PIXELS], U8, align_bytes=64)
@@ -274,8 +283,9 @@ def tile_memory_sup_pb_v_kernel(
                             in1=query_t[k // HALVES][:, k % HALVES, :],
                             op0=ALU.mult, op1=ALU.mult, accum_out=weight[:, k : k + 1],
                         )
-                    out_sb = stage2.tile([P, GROUP_IMAGES, PACK, IMAGE_PIXELS], F32)
                     for k in range(BLOCKS):
+                        if k % HALVES == 0:
+                            out_sb = stage2.tile([P, PACK, IMAGE_PIXELS], F32, bufs=4)
                         nc.vector.scalar_tensor_tensor(
                             out=scaled[k][:], in0=query_t[k // HALVES][:, k % HALVES, :], scalar=weight[:, k : k + 1],
                             in1=scaled[k][:], op0=ALU.mult, op1=ALU.add,
@@ -284,5 +294,9 @@ def tile_memory_sup_pb_v_kernel(
                         for t in range(PACK):
                             nc.tensor.transpose(out_t[:, t, :], scaled[k][:, t * P : (t + 1) * P], ident_f32[:])
                         first = (k % HALVES) * P
-                        nc.scalar.copy(out=out_sb[:, k // HALVES, :, first : first + P], in_=out_t[:])
-                    nc.sync.dma_start(out=out_groups[g], in_=out_sb[:].rearrange("p b t n -> p b (t n)"))
+                        nc.scalar.copy(out=out_sb[:, :, first : first + P], in_=out_t[:])
+                        if k % HALVES == HALVES - 1:
+                            nc.sync.dma_start(
+                                out=out_images[g * GROUP_IMAGES + k // HALVES],
+                                in_=out_sb[:].rearrange("p t n -> p (t n)"),
+                            )

@@ -47,17 +47,17 @@ def tile_memory_sup_pb_v_kernel(
     y_groups = y_conv.rearrange("(g k p) o -> g p k o", k=BLOCKS, p=P)
     grad_groups = grad_out.rearrange("(g b) (p t) h w -> g p b (t h w)", b=GROUP_IMAGES, t=PACK)
     query_groups = query.rearrange("(g b) (p t) h w -> g p b (t h w)", b=GROUP_IMAGES, t=PACK)
-    out_images = out.rearrange("b (p t) h w -> b p (t h w)", t=PACK)
+    out_images = out.rearrange("b (p t) h w -> b p t (h w)", t=PACK)
 
     with tc.tile_pool(name="const", bufs=1) as const, tc.tile_pool(name="resident", bufs=1) as resident:
         var = const.tile([P, PACK], F32)
         mean = const.tile([P, PACK], F32)
         gamma_bf = const.tile([P, PACK], BF16)
         beta_bf = const.tile([P, PACK], BF16)
-        nc.scalar.dma_start(out=var[:], in_=bn_var.rearrange("(p t) -> p t", t=PACK))
-        nc.scalar.dma_start(out=gamma_bf[:], in_=bn_gamma.rearrange("(p t) -> p t", t=PACK))
-        nc.scalar.dma_start(out=mean[:], in_=bn_mean.rearrange("(p t) -> p t", t=PACK))
-        nc.scalar.dma_start(out=beta_bf[:], in_=bn_beta.rearrange("(p t) -> p t", t=PACK))
+        nc.sync.dma_start(out=var[:], in_=bn_var.rearrange("(p t) -> p t", t=PACK))
+        nc.sync.dma_start(out=gamma_bf[:], in_=bn_gamma.rearrange("(p t) -> p t", t=PACK))
+        nc.sync.dma_start(out=mean[:], in_=bn_mean.rearrange("(p t) -> p t", t=PACK))
+        nc.sync.dma_start(out=beta_bf[:], in_=bn_beta.rearrange("(p t) -> p t", t=PACK))
         w_rows = const.tile([P, PACK, CHANNELS], BF16)
 
         ident_f32 = const.tile([P, P], F32)
@@ -106,8 +106,8 @@ def tile_memory_sup_pb_v_kernel(
         nc.vector.tensor_mul(out=sum2_to_slope[:], in0=sum1_to_offset[:], in1=rstd[:])
         nc.vector.tensor_mul(out=sum2_to_slope[:], in0=sum2_to_slope[:], in1=rstd[:])
 
-        sum1_parts = const.tile([P, PACK, GROUPS], F32)
-        sum2_parts = const.tile([P, PACK, GROUPS], F32)
+        sum1_parts = const.tile([P, PACK, GROUPS + GROUP_IMAGES - 1], F32)
+        sum2_parts = const.tile([P, PACK, GROUPS + GROUP_IMAGES - 1], F32)
         norm2 = const.tile([P, GROUPS * BLOCKS], F32)
 
         ds = []
@@ -116,8 +116,8 @@ def tile_memory_sup_pb_v_kernel(
 
         with tc.tile_pool(name="stage1", bufs=3) as stage1, tc.psum_pool(name="psum1", bufs=4) as psum1:
             for g in range(GROUPS):
+                chunks = [(b, 1) for b in range(GROUP_IMAGES)] if g == 0 else [(0, GROUP_IMAGES)]
                 y_sb = stage1.tile([P, BLOCKS, CHANNELS], F32)
-                nc.sync.dma_start(out=y_sb[:], in_=y_groups[g])
                 member = g % PAIR
                 if member == 0:
                     masked_pair = resident.tile(
@@ -128,7 +128,13 @@ def tile_memory_sup_pb_v_kernel(
                     ds.append(ds_pair)
                 masked_g = masked_pair[:, member * GROUP_IMAGES : (member + 1) * GROUP_IMAGES, :, :]
                 ds_g = ds_pair[:, :, member * GROUP_PIXELS : (member + 1) * GROUP_PIXELS]
-                nc.sync.dma_start(out=masked_g.rearrange("p b t n -> p b (t n)"), in_=grad_groups[g])
+                for first, count in chunks:
+                    blocks = slice(first * HALVES, (first + count) * HALVES)
+                    nc.sync.dma_start(out=y_sb[:, blocks, :], in_=y_groups[g][:, blocks, :])
+                    nc.sync.dma_start(
+                        out=masked_g[:, first : first + count, :, :].rearrange("p b t n -> p b (t n)"),
+                        in_=grad_groups[g][:, first : first + count, :],
+                    )
                 query_g = resident.tile([P, GROUP_IMAGES, PACK, IMAGE_PIXELS], BF16, name="query%d" % g)
                 nc.sync.dma_start(out=query_g[:].rearrange("p b t n -> p b (t n)"), in_=query_groups[g])
                 query_sb.append(query_g)
@@ -138,33 +144,39 @@ def tile_memory_sup_pb_v_kernel(
                     )
 
                 y_by_slot = y_sb[:].rearrange("p k (c t) -> p k t c", t=PACK)
-                for t in range(PACK):
-                    y_t = psum1.tile([P, GROUP_PIXELS], F32, tag="y_t")
-                    for k in range(BLOCKS):
-                        nc.tensor.transpose(y_t[:, k * P : (k + 1) * P], y_by_slot[:, k, t, :], ident_f32[:])
-                    nc.scalar.activation(
-                        out=ds_g[:, t, :], in_=y_t[:], func=ACT.Identity,
-                        bias=shift[:, t : t + 1], scale=sign[:, t : t + 1],
-                    )
-                for t in range(PACK):
-                    nc.vector.scalar_tensor_tensor(
-                        out=masked_g[:, :, t, :],
-                        in0=ds_g[:, t, :].rearrange("p (b n) -> p b n", b=GROUP_IMAGES),
-                        scalar=threshold[:, t : t + 1],
-                        in1=masked_g[:, :, t, :],
-                        op0=ALU.is_gt, op1=ALU.mult,
-                        accum_out=sum1_parts[:, t, g : g + 1],
-                    )
-                for t in range(PACK):
-                    product = stage1.tile([P, GROUP_IMAGES, IMAGE_PIXELS], BF16, tag="product", bufs=4)
-                    nc.vector.scalar_tensor_tensor(
-                        out=product[:],
-                        in0=ds_g[:, t, :].rearrange("p (b n) -> p b n", b=GROUP_IMAGES),
-                        scalar=1.0,
-                        in1=masked_g[:, :, t, :],
-                        op0=ALU.mult, op1=ALU.mult,
-                        accum_out=sum2_parts[:, t, g : g + 1],
-                    )
+                for first, count in chunks:
+                    part = g + first + (0 if g == 0 else GROUP_IMAGES - 1)
+                    images = slice(first, first + count)
+                    pixels = slice(first * IMAGE_PIXELS, (first + count) * IMAGE_PIXELS)
+                    for t in range(PACK):
+                        y_t = psum1.tile([P, count * IMAGE_PIXELS], F32, tag="y_t")
+                        for k in range(count * HALVES):
+                            nc.tensor.transpose(
+                                y_t[:, k * P : (k + 1) * P], y_by_slot[:, first * HALVES + k, t, :], ident_f32[:]
+                            )
+                        nc.scalar.activation(
+                            out=ds_g[:, t, pixels], in_=y_t[:], func=ACT.Identity,
+                            bias=shift[:, t : t + 1], scale=sign[:, t : t + 1],
+                        )
+                    for t in range(PACK):
+                        nc.vector.scalar_tensor_tensor(
+                            out=masked_g[:, images, t, :],
+                            in0=ds_g[:, t, pixels].rearrange("p (b n) -> p b n", b=count),
+                            scalar=threshold[:, t : t + 1],
+                            in1=masked_g[:, images, t, :],
+                            op0=ALU.is_gt, op1=ALU.mult,
+                            accum_out=sum1_parts[:, t, part : part + 1],
+                        )
+                    for t in range(PACK):
+                        product = stage1.tile([P, count, IMAGE_PIXELS], BF16, tag="product", bufs=4)
+                        nc.vector.scalar_tensor_tensor(
+                            out=product[:],
+                            in0=ds_g[:, t, pixels].rearrange("p (b n) -> p b n", b=count),
+                            scalar=1.0,
+                            in1=masked_g[:, images, t, :],
+                            op0=ALU.mult, op1=ALU.mult,
+                            accum_out=sum2_parts[:, t, part : part + 1],
+                        )
 
                 for b in range(GROUP_IMAGES):
                     query_t = psum1.tile([P, HALVES, CHANNELS], BF16, tag="query_t")
@@ -295,8 +307,10 @@ def tile_memory_sup_pb_v_kernel(
                             nc.tensor.transpose(out_t[:, t, :], scaled[k][:, t * P : (t + 1) * P], ident_f32[:])
                         first = (k % HALVES) * P
                         nc.scalar.copy(out=out_sb[:, :, first : first + P], in_=out_t[:])
-                        if k % HALVES == HALVES - 1:
+                        image = g * GROUP_IMAGES + k // HALVES
+                        if image == IMAGES - 1:
                             nc.sync.dma_start(
-                                out=out_images[g * GROUP_IMAGES + k // HALVES],
-                                in_=out_sb[:].rearrange("p t n -> p (t n)"),
+                                out=out_images[image][:, :, first : first + P], in_=out_sb[:, :, first : first + P]
                             )
+                        elif k % HALVES == HALVES - 1:
+                            nc.sync.dma_start(out=out_images[image], in_=out_sb[:])

@@ -22,7 +22,7 @@ GROUP_PIXELS = GROUP_IMAGES * IMAGE_PIXELS
 GROUPS = IMAGES // GROUP_IMAGES
 PAIR = 2
 W_LOAD_AFTER_GROUP = 2
-VECTOR_SHARE = 640
+VECTOR_SHARE = 576
 HALVES = IMAGE_PIXELS // P
 BLOCKS = GROUP_PIXELS // P
 BN_EPS = 1e-5
@@ -228,10 +228,17 @@ def tile_memory_sup_pb_v_kernel(
             for pair in range(GROUPS // PAIR):
                 members = [pair * PAIR + i for i in range(PAIR)]
                 for t in range(PACK):
-                    nc.scalar.activation(
-                        out=ds[pair][:, t, :], in_=ds[pair][:, t, :], func=ACT.Identity,
-                        bias=offset[:, t : t + 1], scale=slope[:, t : t + 1],
-                    )
+                    if pair == 0 and t == 0:
+                        nc.vector.tensor_scalar(
+                            out=ds[pair][:, t, :], in0=ds[pair][:, t, :],
+                            scalar1=slope[:, t : t + 1], scalar2=offset[:, t : t + 1],
+                            op0=ALU.mult, op1=ALU.add,
+                        )
+                    else:
+                        nc.scalar.activation(
+                            out=ds[pair][:, t, :], in_=ds[pair][:, t, :], func=ACT.Identity,
+                            bias=offset[:, t : t + 1], scale=slope[:, t : t + 1],
+                        )
                 dy_rows = stage2.tile([P, PACK, PAIR * GROUP_PIXELS], BF16)
                 for t in range(PACK):
                     nc.vector.scalar_tensor_tensor(

@@ -254,8 +254,8 @@ def tile_memory_sup_pb_v_kernel(
                     in_=dy_rows[:, :, 0:VECTOR_SHARE].rearrange("p t (c i) -> p c t i", i=4),
                 )
                 nc.scalar.copy(
-                    out=dy_words_bf[:, VECTOR_SHARE:, :],
-                    in_=dy_rows[:, :, VECTOR_SHARE:].rearrange("p t n -> p n t"),
+                    out=dy_words_bf[:, VECTOR_SHARE:, :].rearrange("p (c i) t -> p c t i", i=4),
+                    in_=dy_rows[:, :, VECTOR_SHARE:].rearrange("p t (c i) -> p c t i", i=4),
                 )
                 dy_codes = stage2.tile([P, PAIR * GROUP_PIXELS], U32, align_bytes=64)
                 dy_scales = stage2.tile([P, PAIR * GROUP_PIXELS], U8, align_bytes=64)

@@ -149,7 +149,7 @@ def tile_memory_sup_pb_v_kernel(
                     images = slice(first, first + count)
                     pixels = slice(first * IMAGE_PIXELS, (first + count) * IMAGE_PIXELS)
                     for t in range(PACK):
-                        y_t = psum1.tile([P, count * IMAGE_PIXELS], F32, tag="y_t")
+                        y_t = psum1.tile([P, count * IMAGE_PIXELS], F32, tag="y_t", bufs=5)
                         for k in range(count * HALVES):
                             nc.tensor.transpose(
                                 y_t[:, k * P : (k + 1) * P], y_by_slot[:, first * HALVES + k, t, :], ident_f32[:]
@@ -179,7 +179,7 @@ def tile_memory_sup_pb_v_kernel(
                         )
 
                 for b in range(GROUP_IMAGES):
-                    query_t = psum1.tile([P, HALVES, CHANNELS], BF16, tag="query_t")
+                    query_t = psum1.tile([P, HALVES, CHANNELS], BF16, tag="query_t", bufs=3)
                     for h in range(HALVES):
                         for t in range(PACK):
                             nc.tensor.transpose(

@@ -44,7 +44,8 @@ def tile_memory_sup_pb_v_kernel(
 ):
     nc = tc.nc
 
-    y_groups = y_conv.rearrange("(g k p) o -> g p k o", k=BLOCKS, p=P)
+    y_groups = y_conv.rearrange("(g p k) o -> g p k o", k=BLOCKS, p=P)
+    y_images = y_conv.rearrange("(i p k) o -> i p k o", k=HALVES, p=P)
     grad_groups = grad_out.rearrange("(g b) (p t) h w -> g p b (t h w)", b=GROUP_IMAGES, t=PACK)
     query_groups = query.rearrange("(g b) (p t) h w -> g p b (t h w)", b=GROUP_IMAGES, t=PACK)
     out_images = out.rearrange("b (p t) h w -> b p t (h w)", t=PACK)
@@ -130,7 +131,8 @@ def tile_memory_sup_pb_v_kernel(
                 ds_g = ds_pair[:, :, member * GROUP_PIXELS : (member + 1) * GROUP_PIXELS]
                 for first, count in chunks:
                     blocks = slice(first * HALVES, (first + count) * HALVES)
-                    nc.sync.dma_start(out=y_sb[:, blocks, :], in_=y_groups[g][:, blocks, :])
+                    y_source = y_groups[g] if count == GROUP_IMAGES else y_images[g * GROUP_IMAGES + first]
+                    nc.sync.dma_start(out=y_sb[:, blocks, :], in_=y_source)
                     nc.sync.dma_start(
                         out=masked_g[:, first : first + count, :, :].rearrange("p b t n -> p b (t n)"),
                         in_=grad_groups[g][:, first : first + count, :],
@@ -155,7 +157,8 @@ def tile_memory_sup_pb_v_kernel(
                                 y_t[:, k * P : (k + 1) * P], y_by_slot[:, first * HALVES + k, t, :], ident_f32[:]
                             )
                         nc.scalar.activation(
-                            out=ds_g[:, t, pixels], in_=y_t[:], func=ACT.Identity,
+                            out=ds_g[:, t, pixels].rearrange("q (p k) -> q p k", p=P),
+                            in_=y_t[:].rearrange("q (k p) -> q p k", p=P), func=ACT.Identity,
                             bias=shift[:, t : t + 1], scale=sign[:, t : t + 1],
                         )
                     for t in range(PACK):

@@ -21,8 +21,8 @@ GROUP_IMAGES = 2
 GROUP_PIXELS = GROUP_IMAGES * IMAGE_PIXELS
 GROUPS = IMAGES // GROUP_IMAGES
 PAIR = 2
+FACTORS_AFTER_GROUP = 1
 W_LOAD_AFTER_GROUP = 2
-VECTOR_SHARE = 576
 HALVES = IMAGE_PIXELS // P
 BLOCKS = GROUP_PIXELS // P
 BN_EPS = 1e-5
@@ -55,8 +55,8 @@ def tile_memory_sup_pb_v_kernel(
         mean = const.tile([P, PACK], F32)
         gamma_bf = const.tile([P, PACK], BF16)
         beta_bf = const.tile([P, PACK], BF16)
-        nc.sync.dma_start(out=var[:], in_=bn_var.rearrange("(p t) -> p t", t=PACK))
         nc.sync.dma_start(out=gamma_bf[:], in_=bn_gamma.rearrange("(p t) -> p t", t=PACK))
+        nc.sync.dma_start(out=var[:], in_=bn_var.rearrange("(p t) -> p t", t=PACK))
         nc.sync.dma_start(out=mean[:], in_=bn_mean.rearrange("(p t) -> p t", t=PACK))
         nc.sync.dma_start(out=beta_bf[:], in_=bn_beta.rearrange("(p t) -> p t", t=PACK))
         w_rows = const.tile([P, PACK, CHANNELS], BF16)
@@ -66,46 +66,33 @@ def tile_memory_sup_pb_v_kernel(
         ident_bf16 = const.tile([P, P], BF16)
         make_identity(nc, ident_bf16[:])
 
+        sign = const.tile([P, PACK], F32)
+        nc.vector.tensor_single_scalar(out=sign[:], in_=gamma_bf[:], scalar=0.0, op=ALU.is_lt)
+        nc.vector.scalar_tensor_tensor(
+            out=sign[:], in0=gamma_bf[:], scalar=0.0, in1=sign[:], op0=ALU.is_gt, op1=ALU.subtract
+        )
         var_eps = const.tile([P, PACK], F32)
         nc.vector.tensor_scalar_add(out=var_eps[:], in0=var[:], scalar1=BN_EPS)
         sd_rough = const.tile([P, PACK], F32)
         nc.scalar.sqrt(out=sd_rough[:], in_=var_eps[:])
-        sd = const.tile([P, PACK], F32)
-        nc.vector.reciprocal(out=sd[:], in_=sd_rough[:])
-        nc.vector.tensor_mul(out=sd[:], in0=sd[:], in1=var_eps[:])
-        nc.vector.tensor_add(out=sd[:], in0=sd[:], in1=sd_rough[:])
-        nc.vector.tensor_scalar_mul(out=sd[:], in0=sd[:], scalar1=0.5)
-        rstd = const.tile([P, PACK], F32)
-        nc.vector.reciprocal(out=rstd[:], in_=sd[:])
-
-        gamma = const.tile([P, PACK], F32)
-        nc.vector.tensor_copy(out=gamma[:], in_=gamma_bf[:])
-        sign = const.tile([P, PACK], F32)
-        nc.vector.tensor_single_scalar(out=sign[:], in_=gamma[:], scalar=0.0, op=ALU.is_lt)
+        threshold = const.tile([P, PACK], F32)
         nc.vector.scalar_tensor_tensor(
-            out=sign[:], in0=gamma[:], scalar=0.0, in1=sign[:], op0=ALU.is_gt, op1=ALU.subtract
+            out=threshold[:], in0=gamma_bf[:], scalar=-1.0, in1=gamma_bf[:], op0=ALU.mult, op1=ALU.max
         )
+        nc.vector.tensor_scalar_max(out=threshold[:], in0=threshold[:], scalar1=TINY)
+        nc.vector.reciprocal(out=threshold[:], in_=threshold[:])
         shift = const.tile([P, PACK], F32)
         nc.vector.scalar_tensor_tensor(
             out=shift[:], in0=mean[:], scalar=-1.0, in1=sign[:], op0=ALU.mult, op1=ALU.mult
         )
-        threshold = const.tile([P, PACK], F32)
+        twice_sd = const.tile([P, PACK], F32)
+        nc.vector.reciprocal(out=twice_sd[:], in_=sd_rough[:])
+        nc.vector.tensor_mul(out=twice_sd[:], in0=twice_sd[:], in1=var_eps[:])
+        nc.vector.tensor_add(out=twice_sd[:], in0=twice_sd[:], in1=sd_rough[:])
+        nc.vector.tensor_mul(out=threshold[:], in0=threshold[:], in1=twice_sd[:])
         nc.vector.scalar_tensor_tensor(
-            out=threshold[:], in0=gamma[:], scalar=-1.0, in1=gamma[:], op0=ALU.mult, op1=ALU.max
+            out=threshold[:], in0=beta_bf[:], scalar=-0.5, in1=threshold[:], op0=ALU.mult, op1=ALU.mult
         )
-        nc.vector.tensor_scalar_max(out=threshold[:], in0=threshold[:], scalar1=TINY)
-        nc.vector.reciprocal(out=threshold[:], in_=threshold[:])
-        nc.vector.tensor_mul(out=threshold[:], in0=threshold[:], in1=sd[:])
-        nc.vector.scalar_tensor_tensor(
-            out=threshold[:], in0=beta_bf[:], scalar=-1.0, in1=threshold[:], op0=ALU.mult, op1=ALU.mult
-        )
-        gain = const.tile([P, PACK], F32)
-        nc.vector.tensor_mul(out=gain[:], in0=gamma[:], in1=rstd[:])
-        sum1_to_offset = const.tile([P, PACK], F32)
-        nc.vector.tensor_scalar_mul(out=sum1_to_offset[:], in0=gain[:], scalar1=-1.0 / PIXELS)
-        sum2_to_slope = const.tile([P, PACK], F32)
-        nc.vector.tensor_mul(out=sum2_to_slope[:], in0=sum1_to_offset[:], in1=rstd[:])
-        nc.vector.tensor_mul(out=sum2_to_slope[:], in0=sum2_to_slope[:], in1=rstd[:])
 
         sum1_parts = const.tile([P, PACK, GROUPS + GROUP_IMAGES - 1], F32)
         sum2_parts = const.tile([P, PACK, GROUPS + GROUP_IMAGES - 1], F32)
@@ -198,6 +185,21 @@ def tile_memory_sup_pb_v_kernel(
                             accum_out=norm2[:, block : block + 1],
                         )
 
+                if g == FACTORS_AFTER_GROUP:
+                    half_rstd = const.tile([P, PACK], F32)
+                    nc.vector.reciprocal(out=half_rstd[:], in_=twice_sd[:])
+                    gain = const.tile([P, PACK], F32)
+                    nc.vector.scalar_tensor_tensor(
+                        out=gain[:], in0=gamma_bf[:], scalar=2.0, in1=half_rstd[:], op0=ALU.mult, op1=ALU.mult
+                    )
+                    sum1_to_offset = const.tile([P, PACK], F32)
+                    nc.vector.tensor_scalar_mul(out=sum1_to_offset[:], in0=gain[:], scalar1=-1.0 / PIXELS)
+                    sum2_to_slope = const.tile([P, PACK], F32)
+                    nc.vector.scalar_tensor_tensor(
+                        out=sum2_to_slope[:], in0=half_rstd[:], scalar=4.0, in1=half_rstd[:], op0=ALU.mult, op1=ALU.mult
+                    )
+                    nc.vector.tensor_mul(out=sum2_to_slope[:], in0=sum2_to_slope[:], in1=sum1_to_offset[:])
+
         sum1 = const.tile([P, PACK], F32)
         nc.vector.tensor_reduce(out=sum1[:], in_=sum1_parts[:], axis=AXIS.X, op=ALU.add)
         sum2 = const.tile([P, PACK], F32)
@@ -253,12 +255,8 @@ def tile_memory_sup_pb_v_kernel(
                     )
                 dy_words_bf = stage2.tile([P, PAIR * GROUP_PIXELS, PACK], BF16, align_bytes=64)
                 nc.vector.tensor_copy(
-                    out=dy_words_bf[:, 0:VECTOR_SHARE, :].rearrange("p (c i) t -> p c t i", i=4),
-                    in_=dy_rows[:, :, 0:VECTOR_SHARE].rearrange("p t (c i) -> p c t i", i=4),
-                )
-                nc.scalar.copy(
-                    out=dy_words_bf[:, VECTOR_SHARE:, :].rearrange("p (c i) t -> p c t i", i=4),
-                    in_=dy_rows[:, :, VECTOR_SHARE:].rearrange("p t (c i) -> p c t i", i=4),
+                    out=dy_words_bf[:].rearrange("p (c i) t -> p c t i", i=4),
+                    in_=dy_rows[:].rearrange("p t (c i) -> p c t i", i=4),
                 )
                 dy_codes = stage2.tile([P, PAIR * GROUP_PIXELS], U32, align_bytes=64)
                 dy_scales = stage2.tile([P, PAIR * GROUP_PIXELS], U8, align_bytes=64)
@@ -308,13 +306,29 @@ def tile_memory_sup_pb_v_kernel(
                     for k in range(BLOCKS):
                         if k % HALVES == 0:
                             out_sb = stage2.tile([P, PACK, IMAGE_PIXELS], F32, bufs=4)
-                        nc.vector.scalar_tensor_tensor(
-                            out=scaled[k][:], in0=query_t[k // HALVES][:, k % HALVES, :], scalar=weight[:, k : k + 1],
-                            in1=scaled[k][:], op0=ALU.mult, op1=ALU.add,
-                        )
                         out_t = psum2.tile([P, PACK, P], F32, tag="out_t", bufs=3)
-                        for t in range(PACK):
-                            nc.tensor.transpose(out_t[:, t, :], scaled[k][:, t * P : (t + 1) * P], ident_f32[:])
+                        if k % HALVES == 0 and pair < GROUPS // PAIR - 1:
+                            weighted = stage2.tile([P, CHANNELS], F32, tag="weighted", bufs=4)
+                            nc.scalar.activation(
+                                out=weighted[:], in_=query_t[k // HALVES][:, k % HALVES, :], func=ACT.Copy,
+                                scale=weight[:, k : k + 1],
+                            )
+                            for t in range(PACK):
+                                nc.tensor.matmul(
+                                    out_t[:, t, :], lhsT=scaled[k][:, t * P : (t + 1) * P], rhs=ident_f32[:],
+                                    is_transpose=True, start=True, stop=False,
+                                )
+                                nc.tensor.matmul(
+                                    out_t[:, t, :], lhsT=weighted[:, t * P : (t + 1) * P], rhs=ident_f32[:],
+                                    is_transpose=True, start=False, stop=True,
+                                )
+                        else:
+                            nc.vector.scalar_tensor_tensor(
+                                out=scaled[k][:], in0=query_t[k // HALVES][:, k % HALVES, :], scalar=weight[:, k : k + 1],
+                                in1=scaled[k][:], op0=ALU.mult, op1=ALU.add,
+                            )
+                            for t in range(PACK):
+                                nc.tensor.transpose(out_t[:, t, :], scaled[k][:, t * P : (t + 1) * P], ident_f32[:])
                         first = (k % HALVES) * P
                         nc.scalar.copy(out=out_sb[:, :, first : first + P], in_=out_t[:])
                         image = g * GROUP_IMAGES + k // HALVES

@@ -25,6 +25,7 @@ FACTORS_AFTER_GROUP = 1
 W_LOAD_AFTER_GROUP = 2
 HALVES = IMAGE_PIXELS // P
 BLOCKS = GROUP_PIXELS // P
+TOTAL_BLOCKS = GROUPS * BLOCKS
 BN_EPS = 1e-5
 L2_EPS = 1e-12
 TINY = 1e-30
@@ -210,131 +211,189 @@ def tile_memory_sup_pb_v_kernel(
         nc.vector.tensor_mul(out=slope[:], in0=sum2[:], in1=sum2_to_slope[:])
 
         inv_norm = const.tile([P, GROUPS * BLOCKS], F32)
-        nc.scalar.sqrt(out=inv_norm[:], in_=norm2[:])
-        nc.vector.tensor_scalar_max(out=inv_norm[:], in0=inv_norm[:], scalar1=L2_EPS)
-        nc.vector.reciprocal(out=inv_norm[:], in_=inv_norm[:])
         neg_inv_norm2 = const.tile([P, GROUPS * BLOCKS], F32)
-        nc.vector.scalar_tensor_tensor(
-            out=neg_inv_norm2[:], in0=inv_norm[:], scalar=-1.0, in1=inv_norm[:], op0=ALU.mult, op1=ALU.mult
-        )
 
         w_words_bf = const.tile([P, CHANNELS, PACK], BF16, align_bytes=64)
-        nc.vector.tensor_copy(
-            out=w_words_bf[:].rearrange("p (t c) j -> p t c j", t=PACK),
-            in_=w_rows[:].rearrange("p j (c t) -> p t c j", t=PACK),
-        )
         w_codes = const.tile([P, CHANNELS], U32, align_bytes=64)
         w_scales = const.tile([P, CHANNELS], U8, align_bytes=64)
-        nc.vector.quantize_mx(
-            out=w_codes[:].bitcast(E4M3_X4), scales=w_scales[:], in_=w_words_bf[:].rearrange("p c j -> p (c j)")
-        )
 
-        with tc.tile_pool(name="stage2", bufs=2) as stage2, tc.psum_pool(name="psum2", bufs=2) as psum2:
-            for pair in range(GROUPS // PAIR):
-                members = [pair * PAIR + i for i in range(PAIR)]
-                for t in range(PACK):
-                    if pair == 0 and t == 0:
-                        nc.vector.tensor_scalar(
-                            out=ds[pair][:, t, :], in0=ds[pair][:, t, :],
-                            scalar1=slope[:, t : t + 1], scalar2=offset[:, t : t + 1],
-                            op0=ALU.mult, op1=ALU.add,
-                        )
-                    else:
-                        nc.scalar.activation(
-                            out=ds[pair][:, t, :], in_=ds[pair][:, t, :], func=ACT.Identity,
-                            bias=offset[:, t : t + 1], scale=slope[:, t : t + 1],
-                        )
-                dy_rows = stage2.tile([P, PACK, PAIR * GROUP_PIXELS], BF16)
-                for t in range(PACK):
-                    nc.vector.scalar_tensor_tensor(
-                        out=dy_rows[:, t, :].rearrange("p (b n) -> p b n", n=IMAGE_PIXELS),
-                        in0=masked[pair][:, :, t, :],
-                        scalar=gain[:, t : t + 1],
-                        in1=ds[pair][:, t, :].rearrange("p (b n) -> p b n", n=IMAGE_PIXELS),
+        with (
+            tc.tile_pool(name="stage2", bufs=2) as stage2,
+            tc.psum_pool(name="psum2", bufs=2) as psum2,
+            tc.manual_schedule(),
+        ):
+            dy_rows, dy_words_bf, dy_codes, dy_scales = {}, {}, {}, {}
+            query_t, out_sb = {}, {}
+            dq, scaled, weight, weighted, out_t = {}, {}, {}, {}, {}
+
+            def group_parts(g):
+                pair, member = divmod(g, PAIR)
+                images = slice(member * GROUP_IMAGES, (member + 1) * GROUP_IMAGES)
+                pixels = slice(member * GROUP_PIXELS, (member + 1) * GROUP_PIXELS)
+                return masked[pair][:, images, :, :], ds[pair][:, :, pixels]
+
+            def make_affine(g, t):
+                ds_t = group_parts(g)[1][:, t, :]
+                if g == 0:
+                    nc.vector.tensor_scalar(
+                        out=ds_t, in0=ds_t, scalar1=slope[:, t : t + 1], scalar2=offset[:, t : t + 1],
                         op0=ALU.mult, op1=ALU.add,
                     )
-                dy_words_bf = stage2.tile([P, PAIR * GROUP_PIXELS, PACK], BF16, align_bytes=64)
+                else:
+                    nc.scalar.activation(
+                        out=ds_t, in_=ds_t, func=ACT.Identity, bias=offset[:, t : t + 1], scale=slope[:, t : t + 1]
+                    )
+
+            def make_dy(g, t):
+                if t == 0:
+                    dy_rows[g] = stage2.tile([P, PACK, GROUP_PIXELS], BF16, name="dy_rows")
+                masked_g, ds_g = group_parts(g)
+                nc.vector.scalar_tensor_tensor(
+                    out=dy_rows[g][:, t, :].rearrange("p (b n) -> p b n", n=IMAGE_PIXELS),
+                    in0=masked_g[:, :, t, :],
+                    scalar=gain[:, t : t + 1],
+                    in1=ds_g[:, t, :].rearrange("p (b n) -> p b n", n=IMAGE_PIXELS),
+                    op0=ALU.mult, op1=ALU.add,
+                )
+
+            def regroup_dy(g):
+                dy_words_bf[g] = stage2.tile([P, GROUP_PIXELS, PACK], BF16, align_bytes=64, name="dy_words_bf")
                 nc.vector.tensor_copy(
-                    out=dy_words_bf[:].rearrange("p (c i) t -> p c t i", i=4),
-                    in_=dy_rows[:].rearrange("p t (c i) -> p c t i", i=4),
+                    out=dy_words_bf[g][:].rearrange("p (c i) t -> p c t i", i=4),
+                    in_=dy_rows[g][:].rearrange("p t (c i) -> p c t i", i=4),
                 )
-                dy_codes = stage2.tile([P, PAIR * GROUP_PIXELS], U32, align_bytes=64)
-                dy_scales = stage2.tile([P, PAIR * GROUP_PIXELS], U8, align_bytes=64)
+
+            def quantize_dy(g):
+                dy_codes[g] = stage2.tile([P, GROUP_PIXELS], U32, align_bytes=64, name="dy_codes", bufs=3)
+                dy_scales[g] = stage2.tile([P, GROUP_PIXELS], U8, align_bytes=64, name="dy_scales", bufs=3)
                 nc.vector.quantize_mx(
-                    out=dy_codes[:].bitcast(E5M2_X4), scales=dy_scales[:],
-                    in_=dy_words_bf[:].rearrange("p n t -> p (n t)"),
+                    out=dy_codes[g][:].bitcast(E5M2_X4), scales=dy_scales[g][:],
+                    in_=dy_words_bf[g][:].rearrange("p n t -> p (n t)"),
                 )
 
-                for i, g in enumerate(members):
-                    query_t = []
-                    for b in range(GROUP_IMAGES):
-                        query_t_b = psum2.tile([P, HALVES, CHANNELS], BF16, tag="query_t", bufs=3)
-                        for h in range(HALVES):
-                            for t in range(PACK):
-                                nc.tensor.transpose(
-                                    query_t_b[:, h, t * P : (t + 1) * P],
-                                    query_sb[g][:, b, t, h * P : (h + 1) * P],
-                                    ident_bf16[:],
-                                )
-                        query_t.append(query_t_b)
+            def transpose_query(image):
+                query_t[image] = psum2.tile([P, HALVES, CHANNELS], BF16, name="query_t", bufs=3)
+                g, b = divmod(image, GROUP_IMAGES)
+                for h in range(HALVES):
+                    for t in range(PACK):
+                        nc.tensor.transpose(
+                            query_t[image][:, h, t * P : (t + 1) * P],
+                            query_sb[g][:, b, t, h * P : (h + 1) * P],
+                            ident_bf16[:],
+                        )
 
-                    weight = stage2.tile([P, BLOCKS], F32)
-                    scaled = []
-                    for k in range(BLOCKS):
-                        block = g * BLOCKS + k
-                        first_column = (i * BLOCKS + k) * P
-                        dq = psum2.tile([P, CHANNELS], F32, tag="dq", bufs=2)
-                        nc.tensor.matmul_mx(
-                            out=dq[:],
-                            lhsT=dy_codes[:, first_column : first_column + P].bitcast(E5M2_X4),
-                            lhsT_scale=dy_scales[:, first_column : first_column + P],
-                            rhs=w_codes[:].bitcast(E4M3_X4),
-                            rhs_scale=w_scales[:],
-                            start=True, stop=True,
+            def multiply(block):
+                g, k = divmod(block, BLOCKS)
+                dq[block] = psum2.tile([P, CHANNELS], F32, name="dq", bufs=2)
+                nc.tensor.matmul_mx(
+                    out=dq[block][:],
+                    lhsT=dy_codes[g][:, k * P : (k + 1) * P].bitcast(E5M2_X4),
+                    lhsT_scale=dy_scales[g][:, k * P : (k + 1) * P],
+                    rhs=w_codes[:].bitcast(E4M3_X4),
+                    rhs_scale=w_scales[:],
+                    start=True, stop=True,
+                )
+
+            def query_block(block):
+                return query_t[block // HALVES][:, block % HALVES, :]
+
+            def scale_product(block):
+                scaled[block] = stage2.tile([P, CHANNELS], F32, name="scaled", bufs=6)
+                nc.scalar.activation(
+                    out=scaled[block][:], in_=dq[block][:], func=ACT.Copy, scale=inv_norm[:, block : block + 1]
+                )
+
+            def dot(block):
+                weight[block] = stage2.tile([P, 1], F32, name="weight", bufs=6)
+                product = stage2.tile([P, CHANNELS], BF16, bufs=3)
+                nc.vector.scalar_tensor_tensor(
+                    out=product[:], in0=scaled[block][:], scalar=neg_inv_norm2[:, block : block + 1],
+                    in1=query_block(block), op0=ALU.mult, op1=ALU.mult, accum_out=weight[block][:],
+                )
+
+            def sums_in_psum(block):
+                return block % HALVES == 0 and block < TOTAL_BLOCKS - BLOCKS
+
+            def weigh(block):
+                if sums_in_psum(block):
+                    weighted[block] = stage2.tile([P, CHANNELS], F32, name="weighted", bufs=3)
+                    nc.scalar.activation(
+                        out=weighted[block][:], in_=query_block(block), func=ACT.Copy, scale=weight[block][:]
+                    )
+                else:
+                    nc.vector.scalar_tensor_tensor(
+                        out=scaled[block][:], in0=query_block(block), scalar=weight[block][:],
+                        in1=scaled[block][:], op0=ALU.mult, op1=ALU.add,
+                    )
+
+            def transpose_out(block):
+                out_t[block] = psum2.tile([P, PACK, P], F32, name="out_t", bufs=3)
+                for t in range(PACK):
+                    columns = slice(t * P, (t + 1) * P)
+                    if sums_in_psum(block):
+                        nc.tensor.matmul(
+                            out_t[block][:, t, :], lhsT=scaled[block][:, columns], rhs=ident_f32[:],
+                            is_transpose=True, start=True, stop=False,
                         )
-                        scaled_k = stage2.tile([P, CHANNELS], F32, tag="scaled", bufs=2 * BLOCKS)
-                        nc.scalar.activation(
-                            out=scaled_k[:], in_=dq[:], func=ACT.Copy, scale=inv_norm[:, block : block + 1]
+                        nc.tensor.matmul(
+                            out_t[block][:, t, :], lhsT=weighted[block][:, columns], rhs=ident_f32[:],
+                            is_transpose=True, start=False, stop=True,
                         )
-                        scaled.append(scaled_k)
-                        product = stage2.tile([P, CHANNELS], BF16, tag="product", bufs=4)
-                        nc.vector.scalar_tensor_tensor(
-                            out=product[:], in0=scaled_k[:], scalar=neg_inv_norm2[:, block : block + 1],
-                            in1=query_t[k // HALVES][:, k % HALVES, :],
-                            op0=ALU.mult, op1=ALU.mult, accum_out=weight[:, k : k + 1],
-                        )
-                    for k in range(BLOCKS):
-                        if k % HALVES == 0:
-                            out_sb = stage2.tile([P, PACK, IMAGE_PIXELS], F32, bufs=4)
-                        out_t = psum2.tile([P, PACK, P], F32, tag="out_t", bufs=3)
-                        if k % HALVES == 0 and pair < GROUPS // PAIR - 1:
-                            weighted = stage2.tile([P, CHANNELS], F32, tag="weighted", bufs=4)
-                            nc.scalar.activation(
-                                out=weighted[:], in_=query_t[k // HALVES][:, k % HALVES, :], func=ACT.Copy,
-                                scale=weight[:, k : k + 1],
-                            )
-                            for t in range(PACK):
-                                nc.tensor.matmul(
-                                    out_t[:, t, :], lhsT=scaled[k][:, t * P : (t + 1) * P], rhs=ident_f32[:],
-                                    is_transpose=True, start=True, stop=False,
-                                )
-                                nc.tensor.matmul(
-                                    out_t[:, t, :], lhsT=weighted[:, t * P : (t + 1) * P], rhs=ident_f32[:],
-                                    is_transpose=True, start=False, stop=True,
-                                )
-                        else:
-                            nc.vector.scalar_tensor_tensor(
-                                out=scaled[k][:], in0=query_t[k // HALVES][:, k % HALVES, :], scalar=weight[:, k : k + 1],
-                                in1=scaled[k][:], op0=ALU.mult, op1=ALU.add,
-                            )
-                            for t in range(PACK):
-                                nc.tensor.transpose(out_t[:, t, :], scaled[k][:, t * P : (t + 1) * P], ident_f32[:])
-                        first = (k % HALVES) * P
-                        nc.scalar.copy(out=out_sb[:, :, first : first + P], in_=out_t[:])
-                        image = g * GROUP_IMAGES + k // HALVES
-                        if image == IMAGES - 1:
-                            nc.sync.dma_start(
-                                out=out_images[image][:, :, first : first + P], in_=out_sb[:, :, first : first + P]
-                            )
-                        elif k % HALVES == HALVES - 1:
-                            nc.sync.dma_start(out=out_images[image], in_=out_sb[:])
+                    else:
+                        nc.tensor.transpose(out_t[block][:, t, :], scaled[block][:, columns], ident_f32[:])
+
+            def store(block):
+                image, h = divmod(block, HALVES)
+                if h == 0:
+                    out_sb[image] = stage2.tile([P, PACK, IMAGE_PIXELS], F32, name="out_sb", bufs=4)
+                columns = slice(h * P, (h + 1) * P)
+                nc.scalar.copy(out=out_sb[image][:, :, columns], in_=out_t[block][:])
+                if image == IMAGES - 1:
+                    nc.sync.dma_start(out=out_images[image][:, :, columns], in_=out_sb[image][:, :, columns])
+                elif h == HALVES - 1:
+                    nc.sync.dma_start(out=out_images[image], in_=out_sb[image][:])
+
+            nc.scalar.sqrt(out=inv_norm[:], in_=norm2[:])
+            nc.scalar.copy(
+                out=w_words_bf[:].rearrange("p (t c) j -> p t c j", t=PACK),
+                in_=w_rows[:].rearrange("p j (c t) -> p t c j", t=PACK),
+            )
+
+            def finish_head():
+                nc.vector.tensor_scalar_max(out=inv_norm[:], in0=inv_norm[:], scalar1=L2_EPS)
+                nc.vector.reciprocal(out=inv_norm[:], in_=inv_norm[:])
+                nc.vector.scalar_tensor_tensor(
+                    out=neg_inv_norm2[:], in0=inv_norm[:], scalar=-1.0, in1=inv_norm[:], op0=ALU.mult, op1=ALU.mult
+                )
+                nc.vector.quantize_mx(
+                    out=w_codes[:].bitcast(E4M3_X4), scales=w_scales[:], in_=w_words_bf[:].rearrange("p c j -> p (c j)")
+                )
+
+            def run(stage, index, limit, *slot):
+                if 0 <= index < limit:
+                    stage(index, *slot)
+
+            for step in range(-13, TOTAL_BLOCKS + 4):
+                group, phase = divmod(step, BLOCKS)
+                run(multiply, step, TOTAL_BLOCKS)
+                if step % HALVES == 1:
+                    run(transpose_query, (step + 1) // HALVES, IMAGES)
+                run(transpose_out, step - 3, TOTAL_BLOCKS)
+
+                run(scale_product, step, TOTAL_BLOCKS)
+                run(dot, step - 1, TOTAL_BLOCKS)
+                run(weigh, step - 2, TOTAL_BLOCKS)
+                run(make_affine, group + 3 + (phase == 3), GROUPS, (phase + 1) % PACK)
+                if phase == 3:
+                    run(make_dy, group + 2, GROUPS, 0)
+                    run(make_dy, group + 2, GROUPS, 1)
+                elif phase == 0:
+                    run(make_dy, group + 1, GROUPS, 2)
+                    run(make_dy, group + 1, GROUPS, 3)
+                elif phase == 1:
+                    run(regroup_dy, group + 1, GROUPS)
+                else:
+                    run(quantize_dy, group + 1, GROUPS)
+                if step == -2:
+                    finish_head()
+                run(store, step - 4, TOTAL_BLOCKS)

@@ -285,14 +285,15 @@ def tile_memory_sup_pb_v_kernel(
             def multiply(block):
                 g, k = divmod(block, BLOCKS)
                 dq[block] = psum2.tile([P, CHANNELS], F32, name="dq", bufs=2)
-                nc.tensor.matmul_mx(
-                    out=dq[block][:],
-                    lhsT=dy_codes[g][:, k * P : (k + 1) * P].bitcast(E5M2_X4),
-                    lhsT_scale=dy_scales[g][:, k * P : (k + 1) * P],
-                    rhs=w_codes[:].bitcast(E4M3_X4),
-                    rhs_scale=w_scales[:],
-                    start=True, stop=True,
-                )
+                for repeat in range(2):
+                    nc.tensor.matmul_mx(
+                        out=dq[block][:],
+                        lhsT=dy_codes[g][:, k * P : (k + 1) * P].bitcast(E5M2_X4),
+                        lhsT_scale=dy_scales[g][:, k * P : (k + 1) * P],
+                        rhs=w_codes[:].bitcast(E4M3_X4),
+                        rhs_scale=w_scales[:],
+                        start=True, stop=True,
+                    )
 
             def query_block(block):
                 return query_t[block // HALVES][:, block % HALVES, :]

@@ -21,6 +21,7 @@ GROUP_IMAGES = 2
 GROUP_PIXELS = GROUP_IMAGES * IMAGE_PIXELS
 GROUPS = IMAGES // GROUP_IMAGES
 PAIR = 2
+SCALAR_AFFINE_GROUPS = (1, 2, 3)
 FACTORS_AFTER_GROUP = 1
 W_LOAD_AFTER_GROUP = 2
 HALVES = IMAGE_PIXELS // P
@@ -234,7 +235,7 @@ def tile_memory_sup_pb_v_kernel(
 
             def make_affine(g, t):
                 ds_t = group_parts(g)[1][:, t, :]
-                if g == 0:
+                if g not in SCALAR_AFFINE_GROUPS:
                     nc.vector.tensor_scalar(
                         out=ds_t, in0=ds_t, scalar1=slope[:, t : t + 1], scalar2=offset[:, t : t + 1],
                         op0=ALU.mult, op1=ALU.add,
@@ -313,7 +314,7 @@ def tile_memory_sup_pb_v_kernel(
                 )
 
             def sums_in_psum(block):
-                return block % HALVES == 0 and block < TOTAL_BLOCKS - BLOCKS
+                return block < TOTAL_BLOCKS - BLOCKS
 
             def weigh(block):
                 if sums_in_psum(block):
@@ -374,7 +375,7 @@ def tile_memory_sup_pb_v_kernel(
                 if 0 <= index < limit:
                     stage(index, *slot)
 
-            for step in range(-13, TOTAL_BLOCKS + 4):
+            for step in range(-17, TOTAL_BLOCKS + 4):
                 group, phase = divmod(step, BLOCKS)
                 run(multiply, step, TOTAL_BLOCKS)
                 if step % HALVES == 1:
@@ -384,7 +385,11 @@ def tile_memory_sup_pb_v_kernel(
                 run(scale_product, step, TOTAL_BLOCKS)
                 run(dot, step - 1, TOTAL_BLOCKS)
                 run(weigh, step - 2, TOTAL_BLOCKS)
-                run(make_affine, group + 3 + (phase == 3), GROUPS, (phase + 1) % PACK)
+                if group + 4 + (phase == 3) in SCALAR_AFFINE_GROUPS:
+                    make_affine(group + 4 + (phase == 3), (phase + 1) % PACK)
+                if phase == 2 and group + 2 not in SCALAR_AFFINE_GROUPS:
+                    for t in range(PACK):
+                        run(make_affine, group + 2, GROUPS, t)
                 if phase == 3:
                     run(make_dy, group + 2, GROUPS, 0)
                     run(make_dy, group + 2, GROUPS, 1)

@@ -22,7 +22,8 @@ GROUP_PIXELS = GROUP_IMAGES * IMAGE_PIXELS
 GROUPS = IMAGES // GROUP_IMAGES
 PAIR = 2
 SCALAR_AFFINE_GROUPS = (1, 2, 3)
-FACTORS_AFTER_GROUP = 1
+LOADS_AHEAD = 3
+SQUARE_LAG = 9
 W_LOAD_AFTER_GROUP = 2
 HALVES = IMAGE_PIXELS // P
 BLOCKS = GROUP_PIXELS // P
@@ -98,109 +99,151 @@ def tile_memory_sup_pb_v_kernel(
 
         sum1_parts = const.tile([P, PACK, GROUPS + GROUP_IMAGES - 1], F32)
         sum2_parts = const.tile([P, PACK, GROUPS + GROUP_IMAGES - 1], F32)
+        half_rstd = const.tile([P, PACK], F32)
+        gain = const.tile([P, PACK], F32)
+        sum1_to_offset = const.tile([P, PACK], F32)
+        sum2_to_slope = const.tile([P, PACK], F32)
         norm2 = const.tile([P, GROUPS * BLOCKS], F32)
 
         ds = []
         masked = []
         query_sb = []
 
-        with tc.tile_pool(name="stage1", bufs=3) as stage1, tc.psum_pool(name="psum1", bufs=4) as psum1:
-            for g in range(GROUPS):
-                chunks = [(b, 1) for b in range(GROUP_IMAGES)] if g == 0 else [(0, GROUP_IMAGES)]
-                y_sb = stage1.tile([P, BLOCKS, CHANNELS], F32)
-                member = g % PAIR
-                if member == 0:
-                    masked_pair = resident.tile(
-                        [P, PAIR * GROUP_IMAGES, PACK, IMAGE_PIXELS], BF16, name="masked%d" % (g // PAIR)
-                    )
-                    ds_pair = resident.tile([P, PACK, PAIR * GROUP_PIXELS], F32, name="ds%d" % (g // PAIR))
-                    masked.append(masked_pair)
-                    ds.append(ds_pair)
-                masked_g = masked_pair[:, member * GROUP_IMAGES : (member + 1) * GROUP_IMAGES, :, :]
-                ds_g = ds_pair[:, :, member * GROUP_PIXELS : (member + 1) * GROUP_PIXELS]
-                for first, count in chunks:
-                    blocks = slice(first * HALVES, (first + count) * HALVES)
-                    y_source = y_groups[g] if count == GROUP_IMAGES else y_images[g * GROUP_IMAGES + first]
-                    nc.sync.dma_start(out=y_sb[:, blocks, :], in_=y_source)
-                    nc.sync.dma_start(
-                        out=masked_g[:, first : first + count, :, :].rearrange("p b t n -> p b (t n)"),
-                        in_=grad_groups[g][:, first : first + count, :],
-                    )
+        chunks = [(0, b, 1) for b in range(GROUP_IMAGES)] + [(g, 0, GROUP_IMAGES) for g in range(1, GROUPS)]
+        units = [(chunk, t) for chunk in range(len(chunks)) for t in range(PACK)]
+        with (
+            tc.tile_pool(name="stage1", bufs=3) as stage1,
+            tc.psum_pool(name="psum1", bufs=4) as psum1,
+            tc.manual_schedule(),
+        ):
+            y_sb, y_t, query_t1 = {}, {}, {}
+
+            def load_query(g):
                 query_g = resident.tile([P, GROUP_IMAGES, PACK, IMAGE_PIXELS], BF16, name="query%d" % g)
                 nc.sync.dma_start(out=query_g[:].rearrange("p b t n -> p b (t n)"), in_=query_groups[g])
                 query_sb.append(query_g)
+
+            def load(g):
+                if g % PAIR == 0:
+                    masked.append(
+                        resident.tile([P, PAIR * GROUP_IMAGES, PACK, IMAGE_PIXELS], BF16, name="masked%d" % (g // PAIR))
+                    )
+                    ds.append(resident.tile([P, PACK, PAIR * GROUP_PIXELS], F32, name="ds%d" % (g // PAIR)))
+                y_sb[g] = stage1.tile([P, BLOCKS, CHANNELS], F32, name="y_sb")
+                first_image = (g % PAIR) * GROUP_IMAGES
+                for group, first, count in chunks:
+                    if group == g:
+                        blocks = slice(first * HALVES, (first + count) * HALVES)
+                        y_source = y_groups[g] if count == GROUP_IMAGES else y_images[g * GROUP_IMAGES + first]
+                        nc.sync.dma_start(out=y_sb[g][:, blocks, :], in_=y_source)
+                        images = slice(first_image + first, first_image + first + count)
+                        nc.sync.dma_start(
+                            out=masked[g // PAIR][:, images, :, :].rearrange("p b t n -> p b (t n)"),
+                            in_=grad_groups[g][:, first : first + count, :],
+                        )
+                if g > 0:
+                    load_query(g - 1)
+                if g == GROUPS - 1:
+                    load_query(g)
                 if g == W_LOAD_AFTER_GROUP:
                     nc.sync.dma_start(
                         out=w_rows[:], in_=conv_w[:, 0:CHANNELS].rearrange("(p j) c -> p j c", j=PACK)
                     )
 
-                y_by_slot = y_sb[:].rearrange("p k (c t) -> p k t c", t=PACK)
-                for first, count in chunks:
-                    part = g + first + (0 if g == 0 else GROUP_IMAGES - 1)
-                    images = slice(first, first + count)
-                    pixels = slice(first * IMAGE_PIXELS, (first + count) * IMAGE_PIXELS)
-                    for t in range(PACK):
-                        y_t = psum1.tile([P, count * IMAGE_PIXELS], F32, tag="y_t", bufs=5)
-                        for k in range(count * HALVES):
-                            nc.tensor.transpose(
-                                y_t[:, k * P : (k + 1) * P], y_by_slot[:, first * HALVES + k, t, :], ident_f32[:]
-                            )
-                        nc.scalar.activation(
-                            out=ds_g[:, t, pixels].rearrange("q (p k) -> q p k", p=P),
-                            in_=y_t[:].rearrange("q (k p) -> q p k", p=P), func=ACT.Identity,
-                            bias=shift[:, t : t + 1], scale=sign[:, t : t + 1],
-                        )
-                    for t in range(PACK):
-                        nc.vector.scalar_tensor_tensor(
-                            out=masked_g[:, images, t, :],
-                            in0=ds_g[:, t, pixels].rearrange("p (b n) -> p b n", b=count),
-                            scalar=threshold[:, t : t + 1],
-                            in1=masked_g[:, images, t, :],
-                            op0=ALU.is_gt, op1=ALU.mult,
-                            accum_out=sum1_parts[:, t, part : part + 1],
-                        )
-                    for t in range(PACK):
-                        product = stage1.tile([P, count, IMAGE_PIXELS], BF16, tag="product", bufs=4)
-                        nc.vector.scalar_tensor_tensor(
-                            out=product[:],
-                            in0=ds_g[:, t, pixels].rearrange("p (b n) -> p b n", b=count),
-                            scalar=1.0,
-                            in1=masked_g[:, images, t, :],
-                            op0=ALU.mult, op1=ALU.mult,
-                            accum_out=sum2_parts[:, t, part : part + 1],
-                        )
+            def chunk_parts(chunk, t):
+                g, first, count = chunks[chunk]
+                image = (g % PAIR) * GROUP_IMAGES + first
+                pixels = slice(image * IMAGE_PIXELS, (image + count) * IMAGE_PIXELS)
+                return masked[g // PAIR][:, image : image + count, t, :], ds[g // PAIR][:, t, pixels]
 
-                for b in range(GROUP_IMAGES):
-                    query_t = psum1.tile([P, HALVES, CHANNELS], BF16, tag="query_t", bufs=3)
-                    for h in range(HALVES):
-                        for t in range(PACK):
-                            nc.tensor.transpose(
-                                query_t[:, h, t * P : (t + 1) * P],
-                                query_g[:, b, t, h * P : (h + 1) * P],
-                                ident_bf16[:],
-                            )
-                    for h in range(HALVES):
-                        block = (g * GROUP_IMAGES + b) * HALVES + h
-                        square = stage1.tile([P, CHANNELS], BF16, tag="square", bufs=4)
-                        nc.scalar.activation(
-                            out=square[:], in_=query_t[:, h, :], func=ACT.Square,
-                            accum_out=norm2[:, block : block + 1],
-                        )
+            def transpose_y(unit):
+                chunk, t = units[unit]
+                g, first, count = chunks[chunk]
+                y_by_slot = y_sb[g][:].rearrange("p k (c t) -> p k t c", t=PACK)
+                y_t[unit] = psum1.tile([P, count * IMAGE_PIXELS], F32, name="y_t", bufs=5)
+                for k in range(count * HALVES):
+                    nc.tensor.transpose(
+                        y_t[unit][:, k * P : (k + 1) * P], y_by_slot[:, first * HALVES + k, t, :], ident_f32[:]
+                    )
 
-                if g == FACTORS_AFTER_GROUP:
-                    half_rstd = const.tile([P, PACK], F32)
-                    nc.vector.reciprocal(out=half_rstd[:], in_=twice_sd[:])
-                    gain = const.tile([P, PACK], F32)
-                    nc.vector.scalar_tensor_tensor(
-                        out=gain[:], in0=gamma_bf[:], scalar=2.0, in1=half_rstd[:], op0=ALU.mult, op1=ALU.mult
+            def shift_y(unit):
+                chunk, t = units[unit]
+                nc.scalar.activation(
+                    out=chunk_parts(chunk, t)[1].rearrange("q (p k) -> q p k", p=P),
+                    in_=y_t[unit][:].rearrange("q (k p) -> q p k", p=P), func=ACT.Identity,
+                    bias=shift[:, t : t + 1], scale=sign[:, t : t + 1],
+                )
+
+            def mask_gradient(unit):
+                chunk, t = units[unit]
+                masked_part, ds_part = chunk_parts(chunk, t)
+                nc.vector.scalar_tensor_tensor(
+                    out=masked_part, in0=ds_part.rearrange("p (b n) -> p b n", n=IMAGE_PIXELS),
+                    scalar=threshold[:, t : t + 1], in1=masked_part,
+                    op0=ALU.is_gt, op1=ALU.mult, accum_out=sum1_parts[:, t, chunk : chunk + 1],
+                )
+
+            def sum_product(unit):
+                chunk, t = units[unit]
+                masked_part, ds_part = chunk_parts(chunk, t)
+                product = stage1.tile([P, GROUP_IMAGES, IMAGE_PIXELS], BF16, bufs=4)
+                nc.vector.scalar_tensor_tensor(
+                    out=product[:, 0 : chunks[chunk][2], :],
+                    in0=ds_part.rearrange("p (b n) -> p b n", n=IMAGE_PIXELS),
+                    scalar=1.0, in1=masked_part,
+                    op0=ALU.mult, op1=ALU.mult, accum_out=sum2_parts[:, t, chunk : chunk + 1],
+                )
+
+            def transpose_query1(block):
+                image, h = divmod(block, HALVES)
+                g, b = divmod(image, GROUP_IMAGES)
+                if h == 0:
+                    query_t1[image] = psum1.tile([P, HALVES, CHANNELS], BF16, name="query_t1", bufs=3)
+                for t in range(PACK):
+                    nc.tensor.transpose(
+                        query_t1[image][:, h, t * P : (t + 1) * P],
+                        query_sb[g][:, b, t, h * P : (h + 1) * P],
+                        ident_bf16[:],
                     )
-                    sum1_to_offset = const.tile([P, PACK], F32)
-                    nc.vector.tensor_scalar_mul(out=sum1_to_offset[:], in0=gain[:], scalar1=-1.0 / PIXELS)
-                    sum2_to_slope = const.tile([P, PACK], F32)
-                    nc.vector.scalar_tensor_tensor(
-                        out=sum2_to_slope[:], in0=half_rstd[:], scalar=4.0, in1=half_rstd[:], op0=ALU.mult, op1=ALU.mult
-                    )
-                    nc.vector.tensor_mul(out=sum2_to_slope[:], in0=sum2_to_slope[:], in1=sum1_to_offset[:])
+
+            def square_query(block):
+                image, h = divmod(block, HALVES)
+                square = stage1.tile([P, CHANNELS], BF16, bufs=4)
+                nc.scalar.activation(
+                    out=square[:], in_=query_t1[image][:, h, :], func=ACT.Square, accum_out=norm2[:, block : block + 1]
+                )
+
+            def make_factors():
+                nc.vector.reciprocal(out=half_rstd[:], in_=twice_sd[:])
+                nc.vector.scalar_tensor_tensor(
+                    out=gain[:], in0=gamma_bf[:], scalar=2.0, in1=half_rstd[:], op0=ALU.mult, op1=ALU.mult
+                )
+                nc.vector.tensor_scalar_mul(out=sum1_to_offset[:], in0=gain[:], scalar1=-1.0 / PIXELS)
+                nc.vector.scalar_tensor_tensor(
+                    out=sum2_to_slope[:], in0=half_rstd[:], scalar=4.0, in1=half_rstd[:], op0=ALU.mult, op1=ALU.mult
+                )
+                nc.vector.tensor_mul(out=sum2_to_slope[:], in0=sum2_to_slope[:], in1=sum1_to_offset[:])
+
+            def run1(stage, index, limit):
+                if 0 <= index < limit:
+                    stage(index)
+
+            for g in range(LOADS_AHEAD):
+                load(g)
+            for step in range(TOTAL_BLOCKS + SQUARE_LAG + 1):
+                if step < len(units):
+                    chunk, t = units[step]
+                    g, first, count = chunks[chunk]
+                    if t == 0 and first == 0 and 0 < g <= GROUPS - LOADS_AHEAD:
+                        load(g + LOADS_AHEAD - 1)
+                run1(transpose_y, step, len(units))
+                run1(transpose_query1, step - SQUARE_LAG, TOTAL_BLOCKS)
+                run1(shift_y, step - 1, len(units))
+                run1(square_query, step - SQUARE_LAG - 1, TOTAL_BLOCKS)
+                run1(mask_gradient, step - 2, len(units))
+                run1(sum_product, step - 3, len(units))
+                if step == SQUARE_LAG:
+                    make_factors()
 
         sum1 = const.tile([P, PACK], F32)
         nc.vector.tensor_reduce(out=sum1[:], in_=sum1_parts[:], axis=AXIS.X, op=ALU.add)
@@ -375,7 +418,7 @@ def tile_memory_sup_pb_v_kernel(
                 if 0 <= index < limit:
                     stage(index, *slot)
 
-            for step in range(-17, TOTAL_BLOCKS + 4):
+            for step in range(-13, TOTAL_BLOCKS + 4):
                 group, phase = divmod(step, BLOCKS)
                 run(multiply, step, TOTAL_BLOCKS)
                 if step % HALVES == 1:
@@ -385,8 +428,8 @@ def tile_memory_sup_pb_v_kernel(
                 run(scale_product, step, TOTAL_BLOCKS)
                 run(dot, step - 1, TOTAL_BLOCKS)
                 run(weigh, step - 2, TOTAL_BLOCKS)
-                if group + 4 + (phase == 3) in SCALAR_AFFINE_GROUPS:
-                    make_affine(group + 4 + (phase == 3), (phase + 1) % PACK)
+                if group + 3 + (phase == 3) in SCALAR_AFFINE_GROUPS:
+                    make_affine(group + 3 + (phase == 3), (phase + 1) % PACK)
                 if phase == 2 and group + 2 not in SCALAR_AFFINE_GROUPS:
                     for t in range(PACK):
                         run(make_affine, group + 2, GROUPS, t)

@@ -24,7 +24,6 @@ PAIR = 2
 SCALAR_AFFINE_GROUPS = (1, 2, 3)
 LOADS_AHEAD = 3
 SQUARE_LAG = 9
-W_LOAD_AFTER_GROUP = 2
 HALVES = IMAGE_PIXELS // P
 BLOCKS = GROUP_PIXELS // P
 TOTAL_BLOCKS = GROUPS * BLOCKS
@@ -58,10 +57,10 @@ def tile_memory_sup_pb_v_kernel(
         mean = const.tile([P, PACK], F32)
         gamma_bf = const.tile([P, PACK], BF16)
         beta_bf = const.tile([P, PACK], BF16)
-        nc.sync.dma_start(out=gamma_bf[:], in_=bn_gamma.rearrange("(p t) -> p t", t=PACK))
-        nc.sync.dma_start(out=var[:], in_=bn_var.rearrange("(p t) -> p t", t=PACK))
-        nc.sync.dma_start(out=mean[:], in_=bn_mean.rearrange("(p t) -> p t", t=PACK))
-        nc.sync.dma_start(out=beta_bf[:], in_=bn_beta.rearrange("(p t) -> p t", t=PACK))
+        nc.scalar.dma_start(out=gamma_bf[:], in_=bn_gamma.rearrange("(p t) -> p t", t=PACK))
+        nc.scalar.dma_start(out=var[:], in_=bn_var.rearrange("(p t) -> p t", t=PACK))
+        nc.scalar.dma_start(out=mean[:], in_=bn_mean.rearrange("(p t) -> p t", t=PACK))
+        nc.scalar.dma_start(out=beta_bf[:], in_=bn_beta.rearrange("(p t) -> p t", t=PACK))
         w_rows = const.tile([P, PACK, CHANNELS], BF16)
 
         ident_f32 = const.tile([P, P], F32)
@@ -145,7 +144,6 @@ def tile_memory_sup_pb_v_kernel(
                     load_query(g - 1)
                 if g == GROUPS - 1:
                     load_query(g)
-                if g == W_LOAD_AFTER_GROUP:
                     nc.sync.dma_start(
                         out=w_rows[:], in_=conv_w[:, 0:CHANNELS].rearrange("(p j) c -> p j c", j=PACK)
                     )

@@ -341,7 +341,7 @@ def tile_memory_sup_pb_v_kernel(
                 return query_t[block // HALVES][:, block % HALVES, :]
 
             def scale_product(block):
-                scaled[block] = stage2.tile([P, CHANNELS], F32, name="scaled", bufs=6)
+                scaled[block] = stage2.tile([P, CHANNELS], F32, name="scaled", bufs=7)
                 nc.scalar.activation(
                     out=scaled[block][:], in_=dq[block][:], func=ACT.Copy, scale=inv_norm[:, block : block + 1]
                 )
@@ -359,7 +359,7 @@ def tile_memory_sup_pb_v_kernel(
 
             def weigh(block):
                 if sums_in_psum(block):
-                    weighted[block] = stage2.tile([P, CHANNELS], F32, name="weighted", bufs=3)
+                    weighted[block] = stage2.tile([P, CHANNELS], F32, name="weighted", bufs=4)
                     nc.scalar.activation(
                         out=weighted[block][:], in_=query_block(block), func=ACT.Copy, scale=weight[block][:]
                     )
@@ -416,21 +416,20 @@ def tile_memory_sup_pb_v_kernel(
                 if 0 <= index < limit:
                     stage(index, *slot)
 
-            for step in range(-13, TOTAL_BLOCKS + 4):
+            for step in range(-13, TOTAL_BLOCKS + 5):
                 group, phase = divmod(step, BLOCKS)
                 run(multiply, step, TOTAL_BLOCKS)
                 if step % HALVES == 1:
                     run(transpose_query, (step + 1) // HALVES, IMAGES)
-                run(transpose_out, step - 3, TOTAL_BLOCKS)
+                run(transpose_out, step - 4, TOTAL_BLOCKS)
 
                 run(scale_product, step, TOTAL_BLOCKS)
                 run(dot, step - 1, TOTAL_BLOCKS)
                 run(weigh, step - 2, TOTAL_BLOCKS)
                 if group + 3 + (phase == 3) in SCALAR_AFFINE_GROUPS:
                     make_affine(group + 3 + (phase == 3), (phase + 1) % PACK)
-                if phase == 2 and group + 2 not in SCALAR_AFFINE_GROUPS:
-                    for t in range(PACK):
-                        run(make_affine, group + 2, GROUPS, t)
+                if group + 2 + (phase == 3) not in SCALAR_AFFINE_GROUPS:
+                    run(make_affine, group + 2 + (phase == 3), GROUPS, (phase + 1) % PACK)
                 if phase == 3:
                     run(make_dy, group + 2, GROUPS, 0)
                     run(make_dy, group + 2, GROUPS, 1)
@@ -443,4 +442,4 @@ def tile_memory_sup_pb_v_kernel(
                     run(quantize_dy, group + 1, GROUPS)
                 if step == -2:
                     finish_head()
-                run(store, step - 4, TOTAL_BLOCKS)
+                run(store, step - 5, TOTAL_BLOCKS)

import concourse.mybir as mybir
from concourse.masks import make_identity

F32 = mybir.dt.float32
BF16 = mybir.dt.bfloat16
U32 = mybir.dt.uint32
U8 = mybir.dt.uint8
E4M3_X4 = mybir.dt.float8_e4m3fn_x4
E5M2_X4 = mybir.dt.float8_e5m2_x4
ALU = mybir.AluOpType
ACT = mybir.ActivationFunctionType
AXIS = mybir.AxisListType

P = 128
PACK = 4
IMAGES = 16
CHANNELS = P * PACK
IMAGE_PIXELS = 256
PIXELS = IMAGES * IMAGE_PIXELS
GROUP_IMAGES = 2
GROUP_PIXELS = GROUP_IMAGES * IMAGE_PIXELS
GROUPS = IMAGES // GROUP_IMAGES
PAIR = 2
SCALAR_AFFINE_GROUPS = (1, 2, 3)
LOADS_AHEAD = 3
SQUARE_LAG = 9
HALVES = IMAGE_PIXELS // P
BLOCKS = GROUP_PIXELS // P
TOTAL_BLOCKS = GROUPS * BLOCKS
BN_EPS = 1e-5
L2_EPS = 1e-12
TINY = 1e-30

FLOPS = 2 * PIXELS * CHANNELS * CHANNELS
BYTES = (
    2 * PIXELS * CHANNELS
    + 2 * CHANNELS * CHANNELS
    + 4 * PIXELS * CHANNELS
    + 2 * PIXELS * CHANNELS
    + 4 * PIXELS * CHANNELS
)


def tile_memory_sup_pb_v_kernel(
    tc, query, concat_memory, conv_w, bn_gamma, bn_beta, y_conv, bn_mean, bn_var, grad_out, out
):
    nc = tc.nc

    y_groups = y_conv.rearrange("(g p k) o -> g p k o", k=BLOCKS, p=P)
    y_images = y_conv.rearrange("(i p k) o -> i p k o", k=HALVES, p=P)
    grad_groups = grad_out.rearrange("(g b) (p t) h w -> g p b (t h w)", b=GROUP_IMAGES, t=PACK)
    query_groups = query.rearrange("(g b) (p t) h w -> g p b (t h w)", b=GROUP_IMAGES, t=PACK)
    out_images = out.rearrange("b (p t) h w -> b p t (h w)", t=PACK)

    with tc.tile_pool(name="const", bufs=1) as const, tc.tile_pool(name="resident", bufs=1) as resident:
        var = const.tile([P, PACK], F32)
        mean = const.tile([P, PACK], F32)
        gamma_bf = const.tile([P, PACK], BF16)
        beta_bf = const.tile([P, PACK], BF16)
        nc.scalar.dma_start(out=gamma_bf[:], in_=bn_gamma.rearrange("(p t) -> p t", t=PACK))
        nc.scalar.dma_start(out=var[:], in_=bn_var.rearrange("(p t) -> p t", t=PACK))
        nc.scalar.dma_start(out=mean[:], in_=bn_mean.rearrange("(p t) -> p t", t=PACK))
        nc.scalar.dma_start(out=beta_bf[:], in_=bn_beta.rearrange("(p t) -> p t", t=PACK))
        w_rows = const.tile([P, PACK, CHANNELS], BF16)

        ident_f32 = const.tile([P, P], F32)
        make_identity(nc, ident_f32[:])
        ident_bf16 = const.tile([P, P], BF16)
        make_identity(nc, ident_bf16[:])

        sign = const.tile([P, PACK], F32)
        nc.vector.tensor_single_scalar(out=sign[:], in_=gamma_bf[:], scalar=0.0, op=ALU.is_lt)
        nc.vector.scalar_tensor_tensor(
            out=sign[:], in0=gamma_bf[:], scalar=0.0, in1=sign[:], op0=ALU.is_gt, op1=ALU.subtract
        )
        var_eps = const.tile([P, PACK], F32)
        nc.vector.tensor_scalar_add(out=var_eps[:], in0=var[:], scalar1=BN_EPS)
        sd_rough = const.tile([P, PACK], F32)
        nc.scalar.sqrt(out=sd_rough[:], in_=var_eps[:])
        threshold = const.tile([P, PACK], F32)
        nc.vector.scalar_tensor_tensor(
            out=threshold[:], in0=gamma_bf[:], scalar=-1.0, in1=gamma_bf[:], op0=ALU.mult, op1=ALU.max
        )
        nc.vector.tensor_scalar_max(out=threshold[:], in0=threshold[:], scalar1=TINY)
        nc.vector.reciprocal(out=threshold[:], in_=threshold[:])
        shift = const.tile([P, PACK], F32)
        nc.vector.scalar_tensor_tensor(
            out=shift[:], in0=mean[:], scalar=-1.0, in1=sign[:], op0=ALU.mult, op1=ALU.mult
        )
        twice_sd = const.tile([P, PACK], F32)
        nc.vector.reciprocal(out=twice_sd[:], in_=sd_rough[:])
        nc.vector.tensor_mul(out=twice_sd[:], in0=twice_sd[:], in1=var_eps[:])
        nc.vector.tensor_add(out=twice_sd[:], in0=twice_sd[:], in1=sd_rough[:])
        nc.vector.tensor_mul(out=threshold[:], in0=threshold[:], in1=twice_sd[:])
        nc.vector.scalar_tensor_tensor(
            out=threshold[:], in0=beta_bf[:], scalar=-0.5, in1=threshold[:], op0=ALU.mult, op1=ALU.mult
        )

        sum1_parts = const.tile([P, PACK, GROUPS + GROUP_IMAGES - 1], F32)
        sum2_parts = const.tile([P, PACK, GROUPS + GROUP_IMAGES - 1], F32)
        half_rstd = const.tile([P, PACK], F32)
        gain = const.tile([P, PACK], F32)
        sum1_to_offset = const.tile([P, PACK], F32)
        sum2_to_slope = const.tile([P, PACK], F32)
        norm2 = const.tile([P, GROUPS * BLOCKS], F32)

        ds = []
        masked = []
        query_sb = []

        chunks = [(0, b, 1) for b in range(GROUP_IMAGES)] + [(g, 0, GROUP_IMAGES) for g in range(1, GROUPS)]
        units = [(chunk, t) for chunk in range(len(chunks)) for t in range(PACK)]
        with (
            tc.tile_pool(name="stage1", bufs=3) as stage1,
            tc.psum_pool(name="psum1", bufs=4) as psum1,
            tc.manual_schedule(),
        ):
            y_sb, y_t, query_t1 = {}, {}, {}

            def load_query(g):
                query_g = resident.tile([P, GROUP_IMAGES, PACK, IMAGE_PIXELS], BF16, name="query%d" % g)
                nc.sync.dma_start(out=query_g[:].rearrange("p b t n -> p b (t n)"), in_=query_groups[g])
                query_sb.append(query_g)

            def load(g):
                if g % PAIR == 0:
                    masked.append(
                        resident.tile([P, PAIR * GROUP_IMAGES, PACK, IMAGE_PIXELS], BF16, name="masked%d" % (g // PAIR))
                    )
                    ds.append(resident.tile([P, PACK, PAIR * GROUP_PIXELS], F32, name="ds%d" % (g // PAIR)))
                y_sb[g] = stage1.tile([P, BLOCKS, CHANNELS], F32, name="y_sb")
                first_image = (g % PAIR) * GROUP_IMAGES
                for group, first, count in chunks:
                    if group == g:
                        blocks = slice(first * HALVES, (first + count) * HALVES)
                        y_source = y_groups[g] if count == GROUP_IMAGES else y_images[g * GROUP_IMAGES + first]
                        nc.sync.dma_start(out=y_sb[g][:, blocks, :], in_=y_source)
                        images = slice(first_image + first, first_image + first + count)
                        nc.sync.dma_start(
                            out=masked[g // PAIR][:, images, :, :].rearrange("p b t n -> p b (t n)"),
                            in_=grad_groups[g][:, first : first + count, :],
                        )
                if g > 0:
                    load_query(g - 1)
                if g == GROUPS - 1:
                    load_query(g)
                    nc.sync.dma_start(
                        out=w_rows[:], in_=conv_w[:, 0:CHANNELS].rearrange("(p j) c -> p j c", j=PACK)
                    )

            def chunk_parts(chunk, t):
                g, first, count = chunks[chunk]
                image = (g % PAIR) * GROUP_IMAGES + first
                pixels = slice(image * IMAGE_PIXELS, (image + count) * IMAGE_PIXELS)
                return masked[g // PAIR][:, image : image + count, t, :], ds[g // PAIR][:, t, pixels]

            def transpose_y(unit):
                chunk, t = units[unit]
                g, first, count = chunks[chunk]
                y_by_slot = y_sb[g][:].rearrange("p k (c t) -> p k t c", t=PACK)
                y_t[unit] = psum1.tile([P, count * IMAGE_PIXELS], F32, name="y_t", bufs=5)
                for k in range(count * HALVES):
                    nc.tensor.transpose(
                        y_t[unit][:, k * P : (k + 1) * P], y_by_slot[:, first * HALVES + k, t, :], ident_f32[:]
                    )

            def shift_y(unit):
                chunk, t = units[unit]
                nc.scalar.activation(
                    out=chunk_parts(chunk, t)[1].rearrange("q (p k) -> q p k", p=P),
                    in_=y_t[unit][:].rearrange("q (k p) -> q p k", p=P), func=ACT.Identity,
                    bias=shift[:, t : t + 1], scale=sign[:, t : t + 1],
                )

            def mask_gradient(unit):
                chunk, t = units[unit]
                masked_part, ds_part = chunk_parts(chunk, t)
                nc.vector.scalar_tensor_tensor(
                    out=masked_part, in0=ds_part.rearrange("p (b n) -> p b n", n=IMAGE_PIXELS),
                    scalar=threshold[:, t : t + 1], in1=masked_part,
                    op0=ALU.is_gt, op1=ALU.mult, accum_out=sum1_parts[:, t, chunk : chunk + 1],
                )

            def sum_product(unit):
                chunk, t = units[unit]
                masked_part, ds_part = chunk_parts(chunk, t)
                product = stage1.tile([P, GROUP_IMAGES, IMAGE_PIXELS], BF16, bufs=4)
                nc.vector.scalar_tensor_tensor(
                    out=product[:, 0 : chunks[chunk][2], :],
                    in0=ds_part.rearrange("p (b n) -> p b n", n=IMAGE_PIXELS),
                    scalar=1.0, in1=masked_part,
                    op0=ALU.mult, op1=ALU.mult, accum_out=sum2_parts[:, t, chunk : chunk + 1],
                )

            def transpose_query1(block):
                image, h = divmod(block, HALVES)
                g, b = divmod(image, GROUP_IMAGES)
                if h == 0:
                    query_t1[image] = psum1.tile([P, HALVES, CHANNELS], BF16, name="query_t1", bufs=3)
                for t in range(PACK):
                    nc.tensor.transpose(
                        query_t1[image][:, h, t * P : (t + 1) * P],
                        query_sb[g][:, b, t, h * P : (h + 1) * P],
                        ident_bf16[:],
                    )

            def square_query(block):
                image, h = divmod(block, HALVES)
                square = stage1.tile([P, CHANNELS], BF16, bufs=4)
                nc.scalar.activation(
                    out=square[:], in_=query_t1[image][:, h, :], func=ACT.Square, accum_out=norm2[:, block : block + 1]
                )

            def make_factors():
                nc.vector.reciprocal(out=half_rstd[:], in_=twice_sd[:])
                nc.vector.scalar_tensor_tensor(
                    out=gain[:], in0=gamma_bf[:], scalar=2.0, in1=half_rstd[:], op0=ALU.mult, op1=ALU.mult
                )
                nc.vector.tensor_scalar_mul(out=sum1_to_offset[:], in0=gain[:], scalar1=-1.0 / PIXELS)
                nc.vector.scalar_tensor_tensor(
                    out=sum2_to_slope[:], in0=half_rstd[:], scalar=4.0, in1=half_rstd[:], op0=ALU.mult, op1=ALU.mult
                )
                nc.vector.tensor_mul(out=sum2_to_slope[:], in0=sum2_to_slope[:], in1=sum1_to_offset[:])

            def run1(stage, index, limit):
                if 0 <= index < limit:
                    stage(index)

            for g in range(LOADS_AHEAD):
                load(g)
            for step in range(TOTAL_BLOCKS + SQUARE_LAG + 1):
                if step < len(units):
                    chunk, t = units[step]
                    g, first, count = chunks[chunk]
                    if t == 0 and first == 0 and 0 < g <= GROUPS - LOADS_AHEAD:
                        load(g + LOADS_AHEAD - 1)
                run1(transpose_y, step, len(units))
                run1(transpose_query1, step - SQUARE_LAG, TOTAL_BLOCKS)
                run1(shift_y, step - 1, len(units))
                run1(square_query, step - SQUARE_LAG - 1, TOTAL_BLOCKS)
                run1(mask_gradient, step - 2, len(units))
                run1(sum_product, step - 3, len(units))
                if step == SQUARE_LAG:
                    make_factors()

        sum1 = const.tile([P, PACK], F32)
        nc.vector.tensor_reduce(out=sum1[:], in_=sum1_parts[:], axis=AXIS.X, op=ALU.add)
        sum2 = const.tile([P, PACK], F32)
        nc.vector.tensor_reduce(out=sum2[:], in_=sum2_parts[:], axis=AXIS.X, op=ALU.add)
        offset = const.tile([P, PACK], F32)
        nc.vector.tensor_mul(out=offset[:], in0=sum1[:], in1=sum1_to_offset[:])
        slope = const.tile([P, PACK], F32)
        nc.vector.tensor_mul(out=slope[:], in0=sum2[:], in1=sum2_to_slope[:])

        inv_norm = const.tile([P, GROUPS * BLOCKS], F32)
        neg_inv_norm2 = const.tile([P, GROUPS * BLOCKS], F32)

        w_words_bf = const.tile([P, CHANNELS, PACK], BF16, align_bytes=64)
        w_codes = const.tile([P, CHANNELS], U32, align_bytes=64)
        w_scales = const.tile([P, CHANNELS], U8, align_bytes=64)

        with (
            tc.tile_pool(name="stage2", bufs=2) as stage2,
            tc.psum_pool(name="psum2", bufs=2) as psum2,
            tc.manual_schedule(),
        ):
            dy_rows, dy_words_bf, dy_codes, dy_scales = {}, {}, {}, {}
            query_t, out_sb = {}, {}
            dq, scaled, weight, weighted, out_t = {}, {}, {}, {}, {}

            def group_parts(g):
                pair, member = divmod(g, PAIR)
                images = slice(member * GROUP_IMAGES, (member + 1) * GROUP_IMAGES)
                pixels = slice(member * GROUP_PIXELS, (member + 1) * GROUP_PIXELS)
                return masked[pair][:, images, :, :], ds[pair][:, :, pixels]

            def make_affine(g, t):
                ds_t = group_parts(g)[1][:, t, :]
                if g not in SCALAR_AFFINE_GROUPS:
                    nc.vector.tensor_scalar(
                        out=ds_t, in0=ds_t, scalar1=slope[:, t : t + 1], scalar2=offset[:, t : t + 1],
                        op0=ALU.mult, op1=ALU.add,
                    )
                else:
                    nc.scalar.activation(
                        out=ds_t, in_=ds_t, func=ACT.Identity, bias=offset[:, t : t + 1], scale=slope[:, t : t + 1]
                    )

            def make_dy(g, t):
                if t == 0:
                    dy_rows[g] = stage2.tile([P, PACK, GROUP_PIXELS], BF16, name="dy_rows")
                masked_g, ds_g = group_parts(g)
                nc.vector.scalar_tensor_tensor(
                    out=dy_rows[g][:, t, :].rearrange("p (b n) -> p b n", n=IMAGE_PIXELS),
                    in0=masked_g[:, :, t, :],
                    scalar=gain[:, t : t + 1],
                    in1=ds_g[:, t, :].rearrange("p (b n) -> p b n", n=IMAGE_PIXELS),
                    op0=ALU.mult, op1=ALU.add,
                )

            def regroup_dy(g):
                dy_words_bf[g] = stage2.tile([P, GROUP_PIXELS, PACK], BF16, align_bytes=64, name="dy_words_bf")
                nc.vector.tensor_copy(
                    out=dy_words_bf[g][:].rearrange("p (c i) t -> p c t i", i=4),
                    in_=dy_rows[g][:].rearrange("p t (c i) -> p c t i", i=4),
                )

            def quantize_dy(g):
                dy_codes[g] = stage2.tile([P, GROUP_PIXELS], U32, align_bytes=64, name="dy_codes", bufs=3)
                dy_scales[g] = stage2.tile([P, GROUP_PIXELS], U8, align_bytes=64, name="dy_scales", bufs=3)
                nc.vector.quantize_mx(
                    out=dy_codes[g][:].bitcast(E5M2_X4), scales=dy_scales[g][:],
                    in_=dy_words_bf[g][:].rearrange("p n t -> p (n t)"),
                )

            def transpose_query(image):
                query_t[image] = psum2.tile([P, HALVES, CHANNELS], BF16, name="query_t", bufs=3)
                g, b = divmod(image, GROUP_IMAGES)
                for h in range(HALVES):
                    for t in range(PACK):
                        nc.tensor.transpose(
                            query_t[image][:, h, t * P : (t + 1) * P],
                            query_sb[g][:, b, t, h * P : (h + 1) * P],
                            ident_bf16[:],
                        )

            def multiply(block):
                g, k = divmod(block, BLOCKS)
                dq[block] = psum2.tile([P, CHANNELS], F32, name="dq", bufs=2)
                for repeat in range(2):
                    nc.tensor.matmul_mx(
                        out=dq[block][:],
                        lhsT=dy_codes[g][:, k * P : (k + 1) * P].bitcast(E5M2_X4),
                        lhsT_scale=dy_scales[g][:, k * P : (k + 1) * P],
                        rhs=w_codes[:].bitcast(E4M3_X4),
                        rhs_scale=w_scales[:],
                        start=True, stop=True,
                    )

            def query_block(block):
                return query_t[block // HALVES][:, block % HALVES, :]

            def scale_product(block):
                scaled[block] = stage2.tile([P, CHANNELS], F32, name="scaled", bufs=7)
                nc.scalar.activation(
                    out=scaled[block][:], in_=dq[block][:], func=ACT.Copy, scale=inv_norm[:, block : block + 1]
                )

            def dot(block):
                weight[block] = stage2.tile([P, 1], F32, name="weight", bufs=6)
                product = stage2.tile([P, CHANNELS], BF16, bufs=3)
                nc.vector.scalar_tensor_tensor(
                    out=product[:], in0=scaled[block][:], scalar=neg_inv_norm2[:, block : block + 1],
                    in1=query_block(block), op0=ALU.mult, op1=ALU.mult, accum_out=weight[block][:],
                )

            def sums_in_psum(block):
                return block < TOTAL_BLOCKS - BLOCKS

            def weigh(block):
                if sums_in_psum(block):
                    weighted[block] = stage2.tile([P, CHANNELS], F32, name="weighted", bufs=4)
                    nc.scalar.activation(
                        out=weighted[block][:], in_=query_block(block), func=ACT.Copy, scale=weight[block][:]
                    )
                else:
                    nc.vector.scalar_tensor_tensor(
                        out=scaled[block][:], in0=query_block(block), scalar=weight[block][:],
                        in1=scaled[block][:], op0=ALU.mult, op1=ALU.add,
                    )

            def transpose_out(block):
                out_t[block] = psum2.tile([P, PACK, P], F32, name="out_t", bufs=3)
                for t in range(PACK):
                    columns = slice(t * P, (t + 1) * P)
                    if sums_in_psum(block):
                        nc.tensor.matmul(
                            out_t[block][:, t, :], lhsT=scaled[block][:, columns], rhs=ident_f32[:],
                            is_transpose=True, start=True, stop=False,
                        )
                        nc.tensor.matmul(
                            out_t[block][:, t, :], lhsT=weighted[block][:, columns], rhs=ident_f32[:],
                            is_transpose=True, start=False, stop=True,
                        )
                    else:
                        nc.tensor.transpose(out_t[block][:, t, :], scaled[block][:, columns], ident_f32[:])

            def store(block):
                image, h = divmod(block, HALVES)
                if h == 0:
                    out_sb[image] = stage2.tile([P, PACK, IMAGE_PIXELS], F32, name="out_sb", bufs=4)
                columns = slice(h * P, (h + 1) * P)
                nc.scalar.copy(out=out_sb[image][:, :, columns], in_=out_t[block][:])
                if image == IMAGES - 1:
                    nc.sync.dma_start(out=out_images[image][:, :, columns], in_=out_sb[image][:, :, columns])
                elif h == HALVES - 1:
                    nc.sync.dma_start(out=out_images[image], in_=out_sb[image][:])

            nc.scalar.sqrt(out=inv_norm[:], in_=norm2[:])
            nc.scalar.copy(
                out=w_words_bf[:].rearrange("p (t c) j -> p t c j", t=PACK),
                in_=w_rows[:].rearrange("p j (c t) -> p t c j", t=PACK),
            )

            def finish_head():
                nc.vector.tensor_scalar_max(out=inv_norm[:], in0=inv_norm[:], scalar1=L2_EPS)
                nc.vector.reciprocal(out=inv_norm[:], in_=inv_norm[:])
                nc.vector.scalar_tensor_tensor(
                    out=neg_inv_norm2[:], in0=inv_norm[:], scalar=-1.0, in1=inv_norm[:], op0=ALU.mult, op1=ALU.mult
                )
                nc.vector.quantize_mx(
                    out=w_codes[:].bitcast(E4M3_X4), scales=w_scales[:], in_=w_words_bf[:].rearrange("p c j -> p (c j)")
                )

            def run(stage, index, limit, *slot):
                if 0 <= index < limit:
                    stage(index, *slot)

            for step in range(-13, TOTAL_BLOCKS + 5):
                group, phase = divmod(step, BLOCKS)
                run(multiply, step, TOTAL_BLOCKS)
                if step % HALVES == 1:
                    run(transpose_query, (step + 1) // HALVES, IMAGES)
                run(transpose_out, step - 4, TOTAL_BLOCKS)

                run(scale_product, step, TOTAL_BLOCKS)
                run(dot, step - 1, TOTAL_BLOCKS)
                run(weigh, step - 2, TOTAL_BLOCKS)
                if group + 3 + (phase == 3) in SCALAR_AFFINE_GROUPS:
                    make_affine(group + 3 + (phase == 3), (phase + 1) % PACK)
                if group + 2 + (phase == 3) not in SCALAR_AFFINE_GROUPS:
                    run(make_affine, group + 2 + (phase == 3), GROUPS, (phase + 1) % PACK)
                if phase == 3:
                    run(make_dy, group + 2, GROUPS, 0)
                    run(make_dy, group + 2, GROUPS, 1)
                elif phase == 0:
                    run(make_dy, group + 1, GROUPS, 2)
                    run(make_dy, group + 1, GROUPS, 3)
                elif phase == 1:
                    run(regroup_dy, group + 1, GROUPS)
                else:
                    run(quantize_dy, group + 1, GROUPS)
                if step == -2:
                    finish_head()
                run(store, step - 5, TOTAL_BLOCKS)
